import numpy as np
import ml_dtypes


def mxq(x, axis, fmt="e4m3"):
    dtype, down = {"e4m3": (ml_dtypes.float8_e4m3fn, 7), "e5m2": (ml_dtypes.float8_e5m2, 14)}[fmt]
    v = np.moveaxis(np.asarray(x, np.float32).astype(ml_dtypes.bfloat16).astype(np.float64), axis, -1)
    blocks = v.reshape(v.shape[:-1] + (-1, 32))
    amax = np.abs(blocks).max(-1, keepdims=True)
    byte = np.maximum(np.where(amax > 0, np.frexp(amax)[1] - 1 + 127, 0) - down, 1)
    scale = np.exp2(byte - 127.0)
    codes = (blocks / scale).astype(np.float32).astype(dtype).astype(np.float64)
    return np.moveaxis((codes * scale).reshape(v.shape), -1, axis)


WIDE = False


def mx_kscale(k):
    if not WIDE:
        return np.ones(k)
    levels = np.array([10, -10, 5, -5, 0])
    a = np.random.permutation(np.resize(levels, k // 512 * 4)).reshape(k // 512, 4)
    idx = np.arange(k)
    return np.exp2(a[idx // 512, idx % 128 // 32])


BF16 = ml_dtypes.bfloat16


def bf(x):
    return np.asarray(x, np.float32).astype(BF16)


def f64(x):
    return np.asarray(x).astype(np.float64)


B, T, C, NH, NC = 4, 1024, 512, 4, 2
HS = C // NH
N = T // NC


def setup_inputs():
    s = mx_kscale(T)
    return {"q": bf(np.random.standard_normal((B, NH, T, HS)) * 2.0),
            "k_mix": bf(np.random.standard_normal((B, NH, T, HS))),
            "v_heads": bf(np.random.standard_normal((B, NH, T, HS)) * s[:, None]),
            "pv_W": bf(np.random.standard_normal((NC, N, N)) / np.sqrt(N) / s.reshape(NC, 1, N)),
            "pv_b": bf(np.random.standard_normal((NC, N)) * 0.3)}


def reference(q, k_mix, v_heads, pv_W, pv_b):
    vh = f64(v_heads).reshape(B, NH, NC, N, HS)
    vm = ((mxq(f64(pv_W), 2, "e4m3") @ mxq(vh, 3, "e4m3")) + f64(pv_b)[:, :, None]).reshape(B, NH, T, HS)
    s = f64(q) @ f64(k_mix).transpose(0, 1, 3, 2) / np.sqrt(HS)
    e = np.exp(s - s.max(-1, keepdims=True))
    y = (mxq(e, 3, "e4m3") @ mxq(vm, 2, "e4m3")) / e.sum(-1, keepdims=True)
    return y.transpose(0, 2, 1, 3).reshape(B, T, C)

@@ -1,0 +1,255 @@
+import math
+from contextlib import ExitStack
+
+import concourse.mybir as mybir
+from concourse.masks import make_identity
+
+BF16 = mybir.dt.bfloat16
+F32 = mybir.dt.float32
+U32 = mybir.dt.uint32
+U8 = mybir.dt.uint8
+FP8X4 = mybir.dt.float8_e4m3fn_x4
+ALU = mybir.AluOpType
+ACT = mybir.ActivationFunctionType
+AXIS_X = mybir.AxisListType.X
+
+BATCH, HEADS, TOKENS, CHANNELS = 4, 4, 1024, 128
+CHUNKS, CHUNK = 2, 512
+P = 128
+PACK = 4
+K_PASS = P * PACK
+PASSES = TOKENS // K_PASS
+TILES = TOKENS // P
+BANK = 512
+HALVES = TOKENS // BANK
+ROUND = 4
+VECTOR_EVERY = 8
+SCALE = 1.0 / math.sqrt(CHANNELS)
+
+FLOPS = 2 * BATCH * HEADS * (2 * TOKENS * TOKENS * CHANNELS + CHUNKS * CHUNK * CHUNK * CHANNELS)
+
+
+def block(index, width):
+    return slice(index * width, (index + 1) * width)
+
+
+def tile_causalselfattention_pb_t_kernel(tc, q, k_mix, v_heads, pv_W, pv_b, out):
+    nc = tc.nc
+    with ExitStack() as ctx:
+        const = ctx.enter_context(tc.tile_pool(name="const", bufs=1))
+        raw = ctx.enter_context(tc.tile_pool(name="raw", bufs=1))
+        per_head = ctx.enter_context(tc.tile_pool(name="per_head", bufs=2))
+        per_tile = ctx.enter_context(tc.tile_pool(name="per_tile", bufs=4))
+        per_round = ctx.enter_context(tc.tile_pool(name="per_round", bufs=2))
+        psum_s = ctx.enter_context(tc.psum_pool(name="psum_s", bufs=3))
+        psum_e = ctx.enter_context(tc.psum_pool(name="psum_e", bufs=3))
+        psum_y = ctx.enter_context(tc.psum_pool(name="psum_y", bufs=1))
+        psum_prep = ctx.enter_context(tc.psum_pool(name="psum_prep", bufs=1))
+
+        heads = [(b, h) for b in range(BATCH) for h in range(HEADS)]
+
+        k_rows, q_rows, v_rows = [], [], []
+        w_rows = const.tile([P, CHUNKS, PACK, CHUNK], BF16)
+        b_rows = const.tile([P, P], BF16)
+        nc.vector.memset(b_rows[:], 0.0)
+        for n, (b, h) in enumerate(heads):
+            k_in = raw.tile([P, TILES, CHANNELS], BF16, name="k_in%d" % n)
+            nc.sync.dma_start(out=k_in[:], in_=k_mix[b, h].rearrange("(i p) d -> p i d", p=P))
+            q_in = raw.tile([P, TILES, CHANNELS], BF16, name="q_in%d" % n)
+            nc.sync.dma_start(out=q_in[:], in_=q[b, h].rearrange("(i p) d -> p i d", p=P))
+            if n == 0:
+                nc.sync.dma_start(out=w_rows[:], in_=pv_W.rearrange("c (t p) n -> p c t n", p=P))
+                nc.sync.dma_start(
+                    out=b_rows[0 : CHUNKS * PACK, :], in_=pv_b.rearrange("c (t p) -> (c t) p", p=P)
+                )
+            v_in = raw.tile([P, CHUNKS, PACK, CHANNELS], BF16, name="v_in%d" % n)
+            nc.sync.dma_start(
+                out=v_in[:], in_=v_heads[b, h].rearrange("(c p j) d -> p c j d", c=CHUNKS, j=PACK)
+            )
+            k_rows.append(k_in)
+            q_rows.append(q_in)
+            v_rows.append(v_in)
+
+        ident_bf16 = const.tile([P, P], BF16)
+        make_identity(nc, ident_bf16[:])
+        ident_f32 = const.tile([P, P], F32)
+        make_identity(nc, ident_f32[:])
+
+        bias = const.tile([P, CHUNKS, PACK], F32)
+        w_codes = const.tile([P, CHUNKS * PACK * P], U32, align_bytes=64)
+        w_scales = const.tile([P, CHUNKS * PACK * P], U8, align_bytes=64)
+
+        def prepare_weights():
+            b_flip = psum_prep.tile([P, P], BF16, tag="prep")
+            nc.tensor.transpose(b_flip[:], b_rows[:], ident_bf16[:])
+            nc.vector.tensor_copy(
+                out=bias[:].rearrange("p c t -> p (c t)"), in_=b_flip[:, 0 : CHUNKS * PACK]
+            )
+            w_grouped = const.tile([P, CHUNKS * PACK, P, PACK], BF16, align_bytes=64)
+            w_grouped_words = w_grouped[:].bitcast(F32)
+            for c in range(CHUNKS):
+                for pair in range(PACK // 2):
+                    w_flip = psum_prep.tile([P, 2, 2, P], F32, tag="prep")
+                    for r in range(2):
+                        words = (
+                            w_rows[:, c, 2 * pair + r, :]
+                            .bitcast(F32)
+                            .rearrange("p (w u) -> p u w", u=2)
+                        )
+                        for u in range(2):
+                            nc.tensor.transpose(w_flip[:, r, u, :], words[:, u, :], ident_f32[:])
+                    first = c * PACK + 2 * pair
+                    nc.vector.tensor_copy(
+                        out=w_grouped_words[:, first : first + 2, :, :],
+                        in_=w_flip[:].rearrange("p r u m -> p r m u"),
+                    )
+            nc.vector.quantize_mx(
+                out=w_codes[:].bitcast(FP8X4),
+                scales=w_scales[:],
+                in_=w_grouped[:].rearrange("p a m t -> p (a m t)"),
+            )
+
+        def flip_keys_and_queries(n):
+            kT = per_head.tile([P, TOKENS], BF16)
+            qT = per_head.tile([P, TOKENS], BF16)
+            for rows, flipped in ((k_rows[n], kT), (q_rows[n], qT)):
+                flip = psum_prep.tile([P, TOKENS], BF16, tag="prep")
+                for i in range(TILES):
+                    nc.tensor.transpose(flip[:, block(i, P)], rows[:, i, :], ident_bf16[:])
+                nc.vector.tensor_copy(out=flipped[:], in_=flip[:])
+            return kT, qT
+
+        def mix_values(n):
+            v_grouped = per_head.tile([P, CHUNKS, CHANNELS, PACK], BF16, align_bytes=64)
+            nc.vector.tensor_copy(out=v_grouped[:], in_=v_rows[n][:].rearrange("p c j d -> p c d j"))
+            v_codes = per_head.tile([P, CHUNKS * CHANNELS], U32, align_bytes=64)
+            v_scales = per_head.tile([P, CHUNKS * CHANNELS], U8, align_bytes=64)
+            nc.vector.quantize_mx(
+                out=v_codes[:].bitcast(FP8X4),
+                scales=v_scales[:],
+                in_=v_grouped[:].rearrange("p c d j -> p (c d j)"),
+            )
+            vm_grouped = per_head.tile([P, CHUNKS, CHANNELS, PACK], BF16, align_bytes=64)
+            for c in range(CHUNKS):
+                vm_ps = psum_prep.tile([P, PACK, CHANNELS], F32, tag="prep")
+                for t in range(PACK):
+                    nc.tensor.matmul_mx(
+                        out=vm_ps[:, t, :],
+                        lhsT=w_codes[:, block(c * PACK + t, P)].bitcast(FP8X4),
+                        lhsT_scale=w_scales[:, block(c * PACK + t, P)],
+                        rhs=v_codes[:, block(c, CHANNELS)].bitcast(FP8X4),
+                        rhs_scale=v_scales[:, block(c, CHANNELS)],
+                        start=True,
+                        stop=True,
+                    )
+                nc.vector.tensor_tensor(
+                    out=vm_grouped[:, c],
+                    in0=vm_ps[:].rearrange("p t d -> p d t"),
+                    in1=bias[:, c, :].unsqueeze(1).to_broadcast([P, CHANNELS, PACK]),
+                    op=ALU.add,
+                )
+            vm_codes = per_head.tile([P, PASSES * CHANNELS], U32, align_bytes=64)
+            vm_scales = per_head.tile([P, PASSES * CHANNELS], U8, align_bytes=64)
+            nc.vector.quantize_mx(
+                out=vm_codes[:].bitcast(FP8X4),
+                scales=vm_scales[:],
+                in_=vm_grouped[:].rearrange("p c d t -> p (c d t)"),
+            )
+            return vm_codes, vm_scales
+
+        def softmax_round(r, kT, qT):
+            e_grouped = per_round.tile([P, ROUND, PASSES, P, PACK], BF16, align_bytes=64)
+            row_sums = per_round.tile([P, ROUND], F32)
+            for a in range(ROUND):
+                i = r * ROUND + a
+                neg_s = per_tile.tile([P, TOKENS], F32)
+                lowest = per_tile.tile([P, HALVES], F32)
+                for half in range(HALVES):
+                    s_half = psum_s.tile([P, BANK], F32)
+                    nc.tensor.matmul(
+                        out=s_half[:],
+                        lhsT=qT[:, block(i, P)],
+                        rhs=kT[:, block(half, BANK)],
+                        start=True,
+                        stop=True,
+                    )
+                    nc.vector.tensor_scalar(
+                        out=neg_s[:, block(half, BANK)],
+                        in0=s_half[:],
+                        scalar1=-SCALE,
+                        scalar2=(None if half == 0 else lowest[:, half - 1 : half]),
+                        op0=ALU.mult,
+                        op1=ALU.min,
+                        accum_out=lowest[:, half : half + 1],
+                    )
+                e_rows = per_tile.tile([P, TOKENS], BF16)
+                nc.scalar.activation(
+                    out=e_rows[:],
+                    in_=neg_s[:],
+                    func=ACT.Exp,
+                    bias=lowest[:, HALVES - 1 : HALVES],
+                    scale=-1.0,
+                    accum_out=row_sums[:, a : a + 1],
+                )
+                e_flip = psum_e.tile([P, TILES, P], BF16)
+                for j in range(TILES):
+                    nc.tensor.transpose(e_flip[:, j, :], e_rows[:, block(j, P)], ident_bf16[:])
+                regrouped = e_flip[:].rearrange("p (g t) m -> p g m t", t=PACK)
+                if i % VECTOR_EVERY == VECTOR_EVERY - 1:
+                    nc.vector.tensor_copy(out=e_grouped[:, a], in_=regrouped)
+                else:
+                    nc.scalar.copy(out=e_grouped[:, a], in_=regrouped)
+            return e_grouped, row_sums
+
+        def weighted_sum(n, r, e_grouped, row_sums, vm_codes, vm_scales):
+            b, h = heads[n]
+            e_codes = per_round.tile([P, ROUND * PASSES * P], U32, align_bytes=64)
+            e_scales = per_round.tile([P, ROUND * PASSES * P], U8, align_bytes=64)
+            nc.vector.quantize_mx(
+                out=e_codes[:].bitcast(FP8X4),
+                scales=e_scales[:],
+                in_=e_grouped[:].rearrange("p a g m t -> p (a g m t)"),
+            )
+            y_ps = psum_y.tile([P, ROUND, CHANNELS], F32)
+            for a in range(ROUND):
+                for g in range(PASSES):
+                    nc.tensor.matmul_mx(
+                        out=y_ps[:, a, :],
+                        lhsT=e_codes[:, block(a * PASSES + g, P)].bitcast(FP8X4),
+                        lhsT_scale=e_scales[:, block(a * PASSES + g, P)],
+                        rhs=vm_codes[:, block(g, CHANNELS)].bitcast(FP8X4),
+                        rhs_scale=vm_scales[:, block(g, CHANNELS)],
+                        start=(g == 0),
+                        stop=(g == PASSES - 1),
+                    )
+            inverse = per_round.tile([P, ROUND], F32)
+            nc.vector.reciprocal(out=inverse[:], in_=row_sums[:])
+            y_sb = per_round.tile([P, ROUND, CHANNELS], F32)
+            nc.vector.tensor_tensor(
+                out=y_sb[:],
+                in0=y_ps[:],
+                in1=inverse[:].unsqueeze(2).to_broadcast([P, ROUND, CHANNELS]),
+                op=ALU.mult,
+            )
+            nc.gpsimd.dma_start(
+                out=out[b, block(r, ROUND * P), block(h, CHANNELS)].rearrange(
+                    "(a p) d -> p a d", p=P
+                ),
+                in_=y_sb[:],
+            )
+
+        flipped = flip_keys_and_queries(0)
+        mixed = None
+        for n in range(len(heads)):
+            kT, qT = flipped
+            e_grouped, row_sums = softmax_round(0, kT, qT)
+            if n == 0:
+                prepare_weights()
+                mixed = mix_values(0)
+            vm_codes, vm_scales = mixed
+            weighted_sum(n, 0, e_grouped, row_sums, vm_codes, vm_scales)
+            if n + 1 < len(heads):
+                flipped = flip_keys_and_queries(n + 1)
+                mixed = mix_values(n + 1)
+            e_grouped, row_sums = softmax_round(1, kT, qT)
+            weighted_sum(n, 1, e_grouped, row_sums, vm_codes, vm_scales)

@@ -23,7 +23,7 @@ TILES = TOKENS // P
 BANK = 512
 HALVES = TOKENS // BANK
 ROUND = 4
-VECTOR_EVERY = 8
+AHEAD = 3
 SCALE = 1.0 / math.sqrt(CHANNELS)
 
 FLOPS = 2 * BATCH * HEADS * (2 * TOKENS * TOKENS * CHANNELS + CHUNKS * CHUNK * CHUNK * CHANNELS)
@@ -37,7 +37,7 @@ def tile_causalselfattention_pb_t_kernel(tc, q, k_mix, v_heads, pv_W, pv_b, out)
     nc = tc.nc
     with ExitStack() as ctx:
         const = ctx.enter_context(tc.tile_pool(name="const", bufs=1))
-        raw = ctx.enter_context(tc.tile_pool(name="raw", bufs=1))
+        raw = ctx.enter_context(tc.tile_pool(name="raw", bufs=AHEAD))
         per_head = ctx.enter_context(tc.tile_pool(name="per_head", bufs=2))
         per_tile = ctx.enter_context(tc.tile_pool(name="per_tile", bufs=4))
         per_round = ctx.enter_context(tc.tile_pool(name="per_round", bufs=2))
@@ -48,27 +48,30 @@ def tile_causalselfattention_pb_t_kernel(tc, q, k_mix, v_heads, pv_W, pv_b, out)
 
         heads = [(b, h) for b in range(BATCH) for h in range(HEADS)]
 
-        k_rows, q_rows, v_rows = [], [], []
-        w_rows = const.tile([P, CHUNKS, PACK, CHUNK], BF16)
-        b_rows = const.tile([P, P], BF16)
-        nc.vector.memset(b_rows[:], 0.0)
-        for n, (b, h) in enumerate(heads):
-            k_in = raw.tile([P, TILES, CHANNELS], BF16, name="k_in%d" % n)
+        k_rows, q_rows, v_rows = {}, {}, {}
+
+        def load_head(n):
+            b, h = heads[n]
+            k_in = raw.tile([P, TILES, CHANNELS], BF16)
             nc.sync.dma_start(out=k_in[:], in_=k_mix[b, h].rearrange("(i p) d -> p i d", p=P))
-            q_in = raw.tile([P, TILES, CHANNELS], BF16, name="q_in%d" % n)
+            q_in = raw.tile([P, TILES, CHANNELS], BF16)
             nc.sync.dma_start(out=q_in[:], in_=q[b, h].rearrange("(i p) d -> p i d", p=P))
-            if n == 0:
-                nc.sync.dma_start(out=w_rows[:], in_=pv_W.rearrange("c (t p) n -> p c t n", p=P))
-                nc.sync.dma_start(
-                    out=b_rows[0 : CHUNKS * PACK, :], in_=pv_b.rearrange("c (t p) -> (c t) p", p=P)
-                )
-            v_in = raw.tile([P, CHUNKS, PACK, CHANNELS], BF16, name="v_in%d" % n)
+            v_in = raw.tile([P, CHUNKS, PACK, CHANNELS], BF16)
             nc.sync.dma_start(
                 out=v_in[:], in_=v_heads[b, h].rearrange("(c p j) d -> p c j d", c=CHUNKS, j=PACK)
             )
-            k_rows.append(k_in)
-            q_rows.append(q_in)
-            v_rows.append(v_in)
+            k_rows[n], q_rows[n], v_rows[n] = k_in, q_in, v_in
+
+        load_head(0)
+        w_rows = const.tile([P, CHUNKS, PACK, CHUNK], BF16)
+        nc.sync.dma_start(out=w_rows[:], in_=pv_W.rearrange("c (t p) n -> p c t n", p=P))
+        b_rows = const.tile([P, P], BF16)
+        nc.vector.memset(b_rows[:], 0.0)
+        nc.sync.dma_start(
+            out=b_rows[0 : CHUNKS * PACK, :], in_=pv_b.rearrange("c (t p) -> (c t) p", p=P)
+        )
+        for n in range(1, AHEAD):
+            load_head(n)
 
         ident_bf16 = const.tile([P, P], BF16)
         make_identity(nc, ident_bf16[:])
@@ -116,7 +119,7 @@ def tile_causalselfattention_pb_t_kernel(tc, q, k_mix, v_heads, pv_W, pv_b, out)
                 flip = psum_prep.tile([P, TOKENS], BF16, tag="prep")
                 for i in range(TILES):
                     nc.tensor.transpose(flip[:, block(i, P)], rows[:, i, :], ident_bf16[:])
-                nc.vector.tensor_copy(out=flipped[:], in_=flip[:])
+                nc.scalar.copy(out=flipped[:], in_=flip[:])
             return kT, qT
 
         def mix_values(n):
@@ -194,11 +197,22 @@ def tile_causalselfattention_pb_t_kernel(tc, q, k_mix, v_heads, pv_W, pv_b, out)
                 e_flip = psum_e.tile([P, TILES, P], BF16)
                 for j in range(TILES):
                     nc.tensor.transpose(e_flip[:, j, :], e_rows[:, block(j, P)], ident_bf16[:])
-                regrouped = e_flip[:].rearrange("p (g t) m -> p g m t", t=PACK)
-                if i % VECTOR_EVERY == VECTOR_EVERY - 1:
-                    nc.vector.tensor_copy(out=e_grouped[:, a], in_=regrouped)
+                if a == ROUND - 1:
+                    nc.scalar.copy(
+                        out=e_grouped[:, a],
+                        in_=e_flip[:].rearrange("p (g t) m -> p g m t", t=PACK),
+                    )
                 else:
-                    nc.scalar.copy(out=e_grouped[:, a], in_=regrouped)
+                    e_planes = per_tile.tile([P, TILES, P], BF16)
+                    nc.scalar.copy(out=e_planes[:], in_=e_flip[:])
+                    nc.gpsimd.tensor_scalar(
+                        out=e_grouped[:, a],
+                        in0=e_planes[:].rearrange("p (g t) m -> p g m t", t=PACK),
+                        scalar1=1.0,
+                        scalar2=0.0,
+                        op0=ALU.mult,
+                        op1=ALU.add,
+                    )
             return e_grouped, row_sums
 
         def weighted_sum(n, r, e_grouped, row_sums, vm_codes, vm_scales):
@@ -231,7 +245,7 @@ def tile_causalselfattention_pb_t_kernel(tc, q, k_mix, v_heads, pv_W, pv_b, out)
                 in1=inverse[:].unsqueeze(2).to_broadcast([P, ROUND, CHANNELS]),
                 op=ALU.mult,
             )
-            nc.gpsimd.dma_start(
+            nc.sync.dma_start(
                 out=out[b, block(r, ROUND * P), block(h, CHANNELS)].rearrange(
                     "(a p) d -> p a d", p=P
                 ),
@@ -251,5 +265,7 @@ def tile_causalselfattention_pb_t_kernel(tc, q, k_mix, v_heads, pv_W, pv_b, out)
             if n + 1 < len(heads):
                 flipped = flip_keys_and_queries(n + 1)
                 mixed = mix_values(n + 1)
+            if n + AHEAD < len(heads):
+                load_head(n + AHEAD)
             e_grouped, row_sums = softmax_round(1, kT, qT)
             weighted_sum(n, 1, e_grouped, row_sums, vm_codes, vm_scales)

@@ -24,6 +24,7 @@ BANK = 512
 HALVES = TOKENS // BANK
 ROUND = 4
 AHEAD = 3
+VECTOR_EVERY = 8
 SCALE = 1.0 / math.sqrt(CHANNELS)
 
 FLOPS = 2 * BATCH * HEADS * (2 * TOKENS * TOKENS * CHANNELS + CHUNKS * CHUNK * CHUNK * CHANNELS)
@@ -119,12 +120,15 @@ def tile_causalselfattention_pb_t_kernel(tc, q, k_mix, v_heads, pv_W, pv_b, out)
                 flip = psum_prep.tile([P, TOKENS], BF16, tag="prep")
                 for i in range(TILES):
                     nc.tensor.transpose(flip[:, block(i, P)], rows[:, i, :], ident_bf16[:])
-                nc.scalar.copy(out=flipped[:], in_=flip[:])
+                nc.vector.tensor_copy(out=flipped[:], in_=flip[:])
             return kT, qT
 
-        def mix_values(n):
+        def group_values(n):
             v_grouped = per_head.tile([P, CHUNKS, CHANNELS, PACK], BF16, align_bytes=64)
             nc.vector.tensor_copy(out=v_grouped[:], in_=v_rows[n][:].rearrange("p c j d -> p c d j"))
+            return v_grouped
+
+        def mix_values(v_grouped):
             v_codes = per_head.tile([P, CHUNKS * CHANNELS], U32, align_bytes=64)
             v_scales = per_head.tile([P, CHUNKS * CHANNELS], U8, align_bytes=64)
             nc.vector.quantize_mx(
@@ -153,11 +157,12 @@ def tile_causalselfattention_pb_t_kernel(tc, q, k_mix, v_heads, pv_W, pv_b, out)
                 )
             vm_codes = per_head.tile([P, PASSES * CHANNELS], U32, align_bytes=64)
             vm_scales = per_head.tile([P, PASSES * CHANNELS], U8, align_bytes=64)
-            nc.vector.quantize_mx(
-                out=vm_codes[:].bitcast(FP8X4),
-                scales=vm_scales[:],
-                in_=vm_grouped[:].rearrange("p c d t -> p (c d t)"),
-            )
+            for c in range(CHUNKS):
+                nc.vector.quantize_mx(
+                    out=vm_codes[:, block(c, CHANNELS)].bitcast(FP8X4),
+                    scales=vm_scales[:, block(c, CHANNELS)],
+                    in_=vm_grouped[:, c].rearrange("p d t -> p (d t)"),
+                )
             return vm_codes, vm_scales
 
         def softmax_round(r, kT, qT):
@@ -180,43 +185,42 @@ def tile_causalselfattention_pb_t_kernel(tc, q, k_mix, v_heads, pv_W, pv_b, out)
                         out=neg_s[:, block(half, BANK)],
                         in0=s_half[:],
                         scalar1=-SCALE,
-                        scalar2=(None if half == 0 else lowest[:, half - 1 : half]),
+                        scalar2=None,
                         op0=ALU.mult,
                         op1=ALU.min,
                         accum_out=lowest[:, half : half + 1],
                     )
+                shift = per_tile.tile([P, 1], F32)
+                nc.gpsimd.tensor_scalar(
+                    out=shift[:],
+                    in0=lowest[:, 0:1],
+                    scalar1=lowest[:, 1:2],
+                    scalar2=None,
+                    op0=ALU.min,
+                )
                 e_rows = per_tile.tile([P, TOKENS], BF16)
                 nc.scalar.activation(
                     out=e_rows[:],
                     in_=neg_s[:],
                     func=ACT.Exp,
-                    bias=lowest[:, HALVES - 1 : HALVES],
+                    bias=shift[:, 0:1],
                     scale=-1.0,
                     accum_out=row_sums[:, a : a + 1],
                 )
                 e_flip = psum_e.tile([P, TILES, P], BF16)
                 for j in range(TILES):
                     nc.tensor.transpose(e_flip[:, j, :], e_rows[:, block(j, P)], ident_bf16[:])
-                if a == ROUND - 1:
-                    nc.scalar.copy(
-                        out=e_grouped[:, a],
-                        in_=e_flip[:].rearrange("p (g t) m -> p g m t", t=PACK),
-                    )
+                regrouped = e_flip[:].rearrange("p (g t) m -> p g m t", t=PACK)
+                if i % VECTOR_EVERY == VECTOR_EVERY - 1:
+                    nc.vector.tensor_copy(out=e_grouped[:, a], in_=regrouped)
                 else:
-                    e_planes = per_tile.tile([P, TILES, P], BF16)
-                    nc.scalar.copy(out=e_planes[:], in_=e_flip[:])
-                    nc.gpsimd.tensor_scalar(
-                        out=e_grouped[:, a],
-                        in0=e_planes[:].rearrange("p (g t) m -> p g m t", t=PACK),
-                        scalar1=1.0,
-                        scalar2=0.0,
-                        op0=ALU.mult,
-                        op1=ALU.add,
-                    )
+                    nc.scalar.copy(out=e_grouped[:, a], in_=regrouped)
             return e_grouped, row_sums
 
         def weighted_sum(n, r, e_grouped, row_sums, vm_codes, vm_scales):
             b, h = heads[n]
+            inverse = per_round.tile([P, ROUND], F32)
+            nc.vector.reciprocal(out=inverse[:], in_=row_sums[:])
             e_codes = per_round.tile([P, ROUND * PASSES * P], U32, align_bytes=64)
             e_scales = per_round.tile([P, ROUND * PASSES * P], U8, align_bytes=64)
             nc.vector.quantize_mx(
@@ -236,8 +240,6 @@ def tile_causalselfattention_pb_t_kernel(tc, q, k_mix, v_heads, pv_W, pv_b, out)
                         start=(g == 0),
                         stop=(g == PASSES - 1),
                     )
-            inverse = per_round.tile([P, ROUND], F32)
-            nc.vector.reciprocal(out=inverse[:], in_=row_sums[:])
             y_sb = per_round.tile([P, ROUND, CHANNELS], F32)
             nc.vector.tensor_tensor(
                 out=y_sb[:],
@@ -258,13 +260,15 @@ def tile_causalselfattention_pb_t_kernel(tc, q, k_mix, v_heads, pv_W, pv_b, out)
             kT, qT = flipped
             e_grouped, row_sums = softmax_round(0, kT, qT)
             if n == 0:
+                v_grouped = group_values(0)
                 prepare_weights()
-                mixed = mix_values(0)
+                mixed = mix_values(v_grouped)
             vm_codes, vm_scales = mixed
             weighted_sum(n, 0, e_grouped, row_sums, vm_codes, vm_scales)
             if n + 1 < len(heads):
+                v_grouped = group_values(n + 1)
                 flipped = flip_keys_and_queries(n + 1)
-                mixed = mix_values(n + 1)
+                mixed = mix_values(v_grouped)
             if n + AHEAD < len(heads):
                 load_head(n + AHEAD)
             e_grouped, row_sums = softmax_round(1, kT, qT)

@@ -24,7 +24,6 @@ BANK = 512
 HALVES = TOKENS // BANK
 ROUND = 4
 AHEAD = 3
-VECTOR_EVERY = 8
 SCALE = 1.0 / math.sqrt(CHANNELS)
 
 FLOPS = 2 * BATCH * HEADS * (2 * TOKENS * TOKENS * CHANNELS + CHUNKS * CHUNK * CHUNK * CHANNELS)
@@ -65,12 +64,9 @@ def tile_causalselfattention_pb_t_kernel(tc, q, k_mix, v_heads, pv_W, pv_b, out)
 
         load_head(0)
         w_rows = const.tile([P, CHUNKS, PACK, CHUNK], BF16)
-        nc.sync.dma_start(out=w_rows[:], in_=pv_W.rearrange("c (t p) n -> p c t n", p=P))
-        b_rows = const.tile([P, P], BF16)
-        nc.vector.memset(b_rows[:], 0.0)
-        nc.sync.dma_start(
-            out=b_rows[0 : CHUNKS * PACK, :], in_=pv_b.rearrange("c (t p) -> (c t) p", p=P)
-        )
+        nc.sync.dma_start(out=w_rows[:], in_=pv_W.rearrange("c (p t) n -> p c t n", t=PACK))
+        bias = const.tile([P, CHUNKS, PACK], BF16)
+        nc.sync.dma_start(out=bias[:], in_=pv_b.rearrange("c (p t) -> p c t", t=PACK))
         for n in range(1, AHEAD):
             load_head(n)
 
@@ -79,16 +75,10 @@ def tile_causalselfattention_pb_t_kernel(tc, q, k_mix, v_heads, pv_W, pv_b, out)
         ident_f32 = const.tile([P, P], F32)
         make_identity(nc, ident_f32[:])
 
-        bias = const.tile([P, CHUNKS, PACK], F32)
         w_codes = const.tile([P, CHUNKS * PACK * P], U32, align_bytes=64)
         w_scales = const.tile([P, CHUNKS * PACK * P], U8, align_bytes=64)
 
         def prepare_weights():
-            b_flip = psum_prep.tile([P, P], BF16, tag="prep")
-            nc.tensor.transpose(b_flip[:], b_rows[:], ident_bf16[:])
-            nc.vector.tensor_copy(
-                out=bias[:].rearrange("p c t -> p (c t)"), in_=b_flip[:, 0 : CHUNKS * PACK]
-            )
             w_grouped = const.tile([P, CHUNKS * PACK, P, PACK], BF16, align_bytes=64)
             w_grouped_words = w_grouped[:].bitcast(F32)
             for c in range(CHUNKS):
@@ -207,14 +197,19 @@ def tile_causalselfattention_pb_t_kernel(tc, q, k_mix, v_heads, pv_W, pv_b, out)
                     scale=-1.0,
                     accum_out=row_sums[:, a : a + 1],
                 )
-                e_flip = psum_e.tile([P, TILES, P], BF16)
-                for j in range(TILES):
-                    nc.tensor.transpose(e_flip[:, j, :], e_rows[:, block(j, P)], ident_bf16[:])
-                regrouped = e_flip[:].rearrange("p (g t) m -> p g m t", t=PACK)
-                if i % VECTOR_EVERY == VECTOR_EVERY - 1:
-                    nc.vector.tensor_copy(out=e_grouped[:, a], in_=regrouped)
-                else:
-                    nc.scalar.copy(out=e_grouped[:, a], in_=regrouped)
+                e_words = e_rows[:].bitcast(F32).rearrange("p (g w u) -> p g u w", g=PASSES, u=2)
+                e_flip = psum_e.tile([P, PASSES, 2, P], F32)
+                for g in range(PASSES):
+                    for u in range(2):
+                        nc.tensor.transpose(e_flip[:, g, u, :], e_words[:, g, u, :], ident_f32[:])
+                regrouped = e_flip[:].rearrange("p g u m -> p g m u")
+                e_grouped_words = (
+                    e_grouped[:, a]
+                    .rearrange("p g m t -> p (g m t)")
+                    .bitcast(F32)
+                    .rearrange("p (g m u) -> p g m u", g=PASSES, u=2)
+                )
+                nc.scalar.copy(out=e_grouped_words, in_=regrouped)
             return e_grouped, row_sums
 
         def weighted_sum(n, r, e_grouped, row_sums, vm_codes, vm_scales):

@@ -23,7 +23,10 @@ TILES = TOKENS // P
 BANK = 512
 HALVES = TOKENS // BANK
 ROUND = 4
+PAIR = 2
 AHEAD = 3
+LEAD_S = 3
+LEAD_M = 2
 SCALE = 1.0 / math.sqrt(CHANNELS)
 
 FLOPS = 2 * BATCH * HEADS * (2 * TOKENS * TOKENS * CHANNELS + CHUNKS * CHUNK * CHUNK * CHANNELS)
@@ -40,13 +43,14 @@ def tile_causalselfattention_pb_t_kernel(tc, q, k_mix, v_heads, pv_W, pv_b, out)
         raw = ctx.enter_context(tc.tile_pool(name="raw", bufs=AHEAD))
         per_head = ctx.enter_context(tc.tile_pool(name="per_head", bufs=2))
         per_tile = ctx.enter_context(tc.tile_pool(name="per_tile", bufs=4))
-        per_round = ctx.enter_context(tc.tile_pool(name="per_round", bufs=2))
-        psum_s = ctx.enter_context(tc.psum_pool(name="psum_s", bufs=3))
-        psum_e = ctx.enter_context(tc.psum_pool(name="psum_e", bufs=3))
-        psum_y = ctx.enter_context(tc.psum_pool(name="psum_y", bufs=1))
-        psum_prep = ctx.enter_context(tc.psum_pool(name="psum_prep", bufs=1))
+        per_round = ctx.enter_context(tc.tile_pool(name="per_round", bufs=3))
+        psum_s = ctx.enter_context(tc.psum_pool(name="psum_s", bufs=6))
+        psum_e = ctx.enter_context(tc.psum_pool(name="psum_e", bufs=1))
+        psum_misc = ctx.enter_context(tc.psum_pool(name="psum_misc", bufs=1))
 
         heads = [(b, h) for b in range(BATCH) for h in range(HEADS)]
+        tiles = len(heads) * TILES
+        rounds = tiles // ROUND
 
         k_rows, q_rows, v_rows = {}, {}, {}
 
@@ -75,155 +79,210 @@ def tile_causalselfattention_pb_t_kernel(tc, q, k_mix, v_heads, pv_W, pv_b, out)
         ident_f32 = const.tile([P, P], F32)
         make_identity(nc, ident_f32[:])
 
+        w_grouped = const.tile([P, CHUNKS * PACK, P, PACK], BF16, align_bytes=64)
         w_codes = const.tile([P, CHUNKS * PACK * P], U32, align_bytes=64)
         w_scales = const.tile([P, CHUNKS * PACK * P], U8, align_bytes=64)
 
-        def prepare_weights():
-            w_grouped = const.tile([P, CHUNKS * PACK, P, PACK], BF16, align_bytes=64)
+        def flip_weights(c, pair):
             w_grouped_words = w_grouped[:].bitcast(F32)
-            for c in range(CHUNKS):
-                for pair in range(PACK // 2):
-                    w_flip = psum_prep.tile([P, 2, 2, P], F32, tag="prep")
-                    for r in range(2):
-                        words = (
-                            w_rows[:, c, 2 * pair + r, :]
-                            .bitcast(F32)
-                            .rearrange("p (w u) -> p u w", u=2)
-                        )
-                        for u in range(2):
-                            nc.tensor.transpose(w_flip[:, r, u, :], words[:, u, :], ident_f32[:])
-                    first = c * PACK + 2 * pair
-                    nc.vector.tensor_copy(
-                        out=w_grouped_words[:, first : first + 2, :, :],
-                        in_=w_flip[:].rearrange("p r u m -> p r m u"),
-                    )
-            nc.vector.quantize_mx(
-                out=w_codes[:].bitcast(FP8X4),
-                scales=w_scales[:],
-                in_=w_grouped[:].rearrange("p a m t -> p (a m t)"),
+            w_flip = psum_misc.tile([P, 2, 2, P], F32, tag="misc")
+            for r in range(2):
+                words = (
+                    w_rows[:, c, 2 * pair + r, :].bitcast(F32).rearrange("p (w u) -> p u w", u=2)
+                )
+                for u in range(2):
+                    nc.tensor.transpose(w_flip[:, r, u, :], words[:, u, :], ident_f32[:])
+            first = c * PACK + 2 * pair
+            nc.vector.tensor_copy(
+                out=w_grouped_words[:, first : first + 2, :, :],
+                in_=w_flip[:].rearrange("p r u m -> p r m u"),
             )
 
-        def flip_keys_and_queries(n):
-            kT = per_head.tile([P, TOKENS], BF16)
-            qT = per_head.tile([P, TOKENS], BF16)
-            for rows, flipped in ((k_rows[n], kT), (q_rows[n], qT)):
-                flip = psum_prep.tile([P, TOKENS], BF16, tag="prep")
-                for i in range(TILES):
-                    nc.tensor.transpose(flip[:, block(i, P)], rows[:, i, :], ident_bf16[:])
-                nc.vector.tensor_copy(out=flipped[:], in_=flip[:])
-            return kT, qT
+        def quantise_weights(c):
+            nc.vector.quantize_mx(
+                out=w_codes[:, block(c, PACK * P)].bitcast(FP8X4),
+                scales=w_scales[:, block(c, PACK * P)],
+                in_=w_grouped[:, block(c, PACK)].rearrange("p a m t -> p (a m t)"),
+            )
+
+        kT, qT, kT_flips, qT_flips = {}, {}, {}, {}
+
+        def flip_rows(n, rows, flips):
+            flip = psum_misc.tile([P, TOKENS], BF16, tag="misc")
+            for i in range(TILES):
+                nc.tensor.transpose(flip[:, block(i, P)], rows[n][:, i, :], ident_bf16[:])
+            flips[n] = flip
+
+        def copy_keys(n, copy):
+            keys = per_head.tile([P, TOKENS], BF16)
+            copy(out=keys[:], in_=kT_flips[n][:])
+            kT[n] = keys
+
+        def copy_queries(n, copy):
+            queries = per_head.tile([P, TOKENS], BF16)
+            copy(out=queries[:], in_=qT_flips[n][:])
+            qT[n] = queries
+
+        v_grouped, v_quantised, vm_banks, vm_grouped, vm_quantised = {}, {}, {}, {}, {}
 
         def group_values(n):
-            v_grouped = per_head.tile([P, CHUNKS, CHANNELS, PACK], BF16, align_bytes=64)
-            nc.vector.tensor_copy(out=v_grouped[:], in_=v_rows[n][:].rearrange("p c j d -> p c d j"))
-            return v_grouped
+            grouped = per_head.tile([P, CHUNKS, CHANNELS, PACK], BF16, align_bytes=64)
+            for c in range(CHUNKS):
+                nc.gpsimd.tensor_scalar(
+                    out=grouped[:, c],
+                    in0=v_rows[n][:, c].rearrange("p j d -> p d j"),
+                    scalar1=1.0,
+                    scalar2=0.0,
+                    op0=ALU.mult,
+                    op1=ALU.add,
+                )
+            v_grouped[n] = grouped
 
-        def mix_values(v_grouped):
+        def quantise_values(n):
             v_codes = per_head.tile([P, CHUNKS * CHANNELS], U32, align_bytes=64)
             v_scales = per_head.tile([P, CHUNKS * CHANNELS], U8, align_bytes=64)
             nc.vector.quantize_mx(
                 out=v_codes[:].bitcast(FP8X4),
                 scales=v_scales[:],
-                in_=v_grouped[:].rearrange("p c d j -> p (c d j)"),
+                in_=v_grouped[n][:].rearrange("p c d j -> p (c d j)"),
             )
-            vm_grouped = per_head.tile([P, CHUNKS, CHANNELS, PACK], BF16, align_bytes=64)
-            for c in range(CHUNKS):
-                vm_ps = psum_prep.tile([P, PACK, CHANNELS], F32, tag="prep")
-                for t in range(PACK):
-                    nc.tensor.matmul_mx(
-                        out=vm_ps[:, t, :],
-                        lhsT=w_codes[:, block(c * PACK + t, P)].bitcast(FP8X4),
-                        lhsT_scale=w_scales[:, block(c * PACK + t, P)],
-                        rhs=v_codes[:, block(c, CHANNELS)].bitcast(FP8X4),
-                        rhs_scale=v_scales[:, block(c, CHANNELS)],
-                        start=True,
-                        stop=True,
-                    )
-                nc.vector.tensor_tensor(
-                    out=vm_grouped[:, c],
-                    in0=vm_ps[:].rearrange("p t d -> p d t"),
-                    in1=bias[:, c, :].unsqueeze(1).to_broadcast([P, CHANNELS, PACK]),
-                    op=ALU.add,
+            v_quantised[n] = (v_codes, v_scales)
+
+        def mix_values(n, c):
+            v_codes, v_scales = v_quantised[n]
+            vm_ps = psum_misc.tile([P, PACK, CHANNELS], F32, tag="misc")
+            for t in range(PACK):
+                nc.tensor.matmul_mx(
+                    out=vm_ps[:, t, :],
+                    lhsT=w_codes[:, block(c * PACK + t, P)].bitcast(FP8X4),
+                    lhsT_scale=w_scales[:, block(c * PACK + t, P)],
+                    rhs=v_codes[:, block(c, CHANNELS)].bitcast(FP8X4),
+                    rhs_scale=v_scales[:, block(c, CHANNELS)],
+                    start=True,
+                    stop=True,
                 )
+            vm_banks[n, c] = vm_ps
+
+        def add_bias(n, c):
+            if c == 0:
+                grouped = per_head.tile([P, CHUNKS, CHANNELS, PACK], BF16, align_bytes=64)
+                vm_grouped[n] = grouped
+            nc.vector.tensor_tensor(
+                out=vm_grouped[n][:, c],
+                in0=vm_banks[n, c][:].rearrange("p t d -> p d t"),
+                in1=bias[:, c, :].unsqueeze(1).to_broadcast([P, CHANNELS, PACK]),
+                op=ALU.add,
+            )
+
+        def quantise_mixed(n):
             vm_codes = per_head.tile([P, PASSES * CHANNELS], U32, align_bytes=64)
             vm_scales = per_head.tile([P, PASSES * CHANNELS], U8, align_bytes=64)
-            for c in range(CHUNKS):
-                nc.vector.quantize_mx(
-                    out=vm_codes[:, block(c, CHANNELS)].bitcast(FP8X4),
-                    scales=vm_scales[:, block(c, CHANNELS)],
-                    in_=vm_grouped[:, c].rearrange("p d t -> p (d t)"),
-                )
-            return vm_codes, vm_scales
-
-        def softmax_round(r, kT, qT):
-            e_grouped = per_round.tile([P, ROUND, PASSES, P, PACK], BF16, align_bytes=64)
-            row_sums = per_round.tile([P, ROUND], F32)
-            for a in range(ROUND):
-                i = r * ROUND + a
-                neg_s = per_tile.tile([P, TOKENS], F32)
-                lowest = per_tile.tile([P, HALVES], F32)
-                for half in range(HALVES):
-                    s_half = psum_s.tile([P, BANK], F32)
-                    nc.tensor.matmul(
-                        out=s_half[:],
-                        lhsT=qT[:, block(i, P)],
-                        rhs=kT[:, block(half, BANK)],
-                        start=True,
-                        stop=True,
-                    )
-                    nc.vector.tensor_scalar(
-                        out=neg_s[:, block(half, BANK)],
-                        in0=s_half[:],
-                        scalar1=-SCALE,
-                        scalar2=None,
-                        op0=ALU.mult,
-                        op1=ALU.min,
-                        accum_out=lowest[:, half : half + 1],
-                    )
-                shift = per_tile.tile([P, 1], F32)
-                nc.gpsimd.tensor_scalar(
-                    out=shift[:],
-                    in0=lowest[:, 0:1],
-                    scalar1=lowest[:, 1:2],
-                    scalar2=None,
-                    op0=ALU.min,
-                )
-                e_rows = per_tile.tile([P, TOKENS], BF16)
-                nc.scalar.activation(
-                    out=e_rows[:],
-                    in_=neg_s[:],
-                    func=ACT.Exp,
-                    bias=shift[:, 0:1],
-                    scale=-1.0,
-                    accum_out=row_sums[:, a : a + 1],
-                )
-                e_words = e_rows[:].bitcast(F32).rearrange("p (g w u) -> p g u w", g=PASSES, u=2)
-                e_flip = psum_e.tile([P, PASSES, 2, P], F32)
-                for g in range(PASSES):
-                    for u in range(2):
-                        nc.tensor.transpose(e_flip[:, g, u, :], e_words[:, g, u, :], ident_f32[:])
-                regrouped = e_flip[:].rearrange("p g u m -> p g m u")
-                e_grouped_words = (
-                    e_grouped[:, a]
-                    .rearrange("p g m t -> p (g m t)")
-                    .bitcast(F32)
-                    .rearrange("p (g m u) -> p g m u", g=PASSES, u=2)
-                )
-                nc.scalar.copy(out=e_grouped_words, in_=regrouped)
-            return e_grouped, row_sums
-
-        def weighted_sum(n, r, e_grouped, row_sums, vm_codes, vm_scales):
-            b, h = heads[n]
-            inverse = per_round.tile([P, ROUND], F32)
-            nc.vector.reciprocal(out=inverse[:], in_=row_sums[:])
-            e_codes = per_round.tile([P, ROUND * PASSES * P], U32, align_bytes=64)
-            e_scales = per_round.tile([P, ROUND * PASSES * P], U8, align_bytes=64)
             nc.vector.quantize_mx(
-                out=e_codes[:].bitcast(FP8X4),
-                scales=e_scales[:],
-                in_=e_grouped[:].rearrange("p a g m t -> p (a g m t)"),
+                out=vm_codes[:].bitcast(FP8X4),
+                scales=vm_scales[:],
+                in_=vm_grouped[n][:].rearrange("p c d t -> p (c d t)"),
             )
-            y_ps = psum_y.tile([P, ROUND, CHANNELS], F32)
+            vm_quantised[n] = (vm_codes, vm_scales)
+
+        s_halves, shifts, e_rows_of, e_flips = {}, {}, {}, {}
+        e_grouped, half_sums, e_quantised = {}, {}, {}
+
+        def scores(n):
+            head, i = divmod(n, TILES)
+            s_halves[n] = []
+            for half in range(HALVES):
+                s_half = psum_s.tile([P, BANK], F32)
+                nc.tensor.matmul(
+                    out=s_half[:],
+                    lhsT=qT[head][:, block(i, P)],
+                    rhs=kT[head][:, block(half, BANK)],
+                    start=True,
+                    stop=True,
+                )
+                s_halves[n].append(s_half)
+
+        def row_maximum(n):
+            highest = per_tile.tile([P, HALVES], F32)
+            for half in range(HALVES):
+                nc.vector.tensor_reduce(
+                    out=highest[:, half : half + 1],
+                    in_=s_halves[n][half][:],
+                    axis=AXIS_X,
+                    op=ALU.max,
+                )
+            shift = per_tile.tile([P, 1], F32)
+            nc.gpsimd.tensor_scalar(
+                out=shift[:],
+                in0=highest[:, 0:1],
+                scalar1=highest[:, 1:2],
+                scalar2=-SCALE,
+                op0=ALU.max,
+                op1=ALU.mult,
+            )
+            shifts[n] = shift
+
+        def exponentials(n):
+            r, a = divmod(n, ROUND)
+            if a == 0:
+                sums = per_round.tile([P, HALVES, ROUND], F32)
+                half_sums[r] = sums
+            e_rows = per_tile.tile([P, TOKENS], BF16)
+            for half in range(HALVES):
+                nc.scalar.activation(
+                    out=e_rows[:, block(half, BANK)],
+                    in_=s_halves[n][half][:],
+                    func=ACT.Exp,
+                    bias=shifts[n][:, 0:1],
+                    scale=SCALE,
+                    accum_out=half_sums[r][:, half, a : a + 1],
+                )
+            e_rows_of[n] = e_rows
+
+        def flip_exponentials(n):
+            words = e_rows_of[n][:].bitcast(F32).rearrange("p (g w u) -> p g u w", g=PASSES, u=2)
+            e_flip = psum_e.tile([P, PASSES, 2, P], F32)
+            for g in range(PASSES):
+                for u in range(2):
+                    nc.tensor.transpose(e_flip[:, g, u, :], words[:, g, u, :], ident_f32[:])
+            e_flips[n] = e_flip
+
+        def regroup_exponentials(n, copy):
+            r, a = divmod(n, ROUND)
+            if a == 0:
+                grouped = per_round.tile([P, ROUND, PASSES, P, PACK], BF16, align_bytes=64)
+                e_grouped[r] = grouped
+            grouped_words = (
+                e_grouped[r][:, a]
+                .rearrange("p g m t -> p (g m t)")
+                .bitcast(F32)
+                .rearrange("p (g m u) -> p g m u", g=PASSES, u=2)
+            )
+            copy(out=grouped_words, in_=e_flips[n][:].rearrange("p g u m -> p g m u"))
+
+        def quantise_exponentials(r, pair):
+            if pair == 0:
+                e_codes = per_round.tile([P, ROUND * PASSES * P], U32, align_bytes=64)
+                e_scales = per_round.tile([P, ROUND * PASSES * P], U8, align_bytes=64)
+                e_quantised[r] = (e_codes, e_scales)
+            e_codes, e_scales = e_quantised[r]
+            width = PAIR * PASSES * P
+            nc.vector.quantize_mx(
+                out=e_codes[:, block(pair, width)].bitcast(FP8X4),
+                scales=e_scales[:, block(pair, width)],
+                in_=e_grouped[r][:, block(pair, PAIR)].rearrange("p a g m t -> p (a g m t)"),
+            )
+
+        sums_of, y_of = {}, {}
+
+        def weighted_sums(r):
+            vm_codes, vm_scales = vm_quantised[r * ROUND // TILES]
+            e_codes, e_scales = e_quantised[r]
+            row_sums = per_round.tile([P, ROUND], F32)
+            nc.gpsimd.tensor_tensor(
+                out=row_sums[:], in0=half_sums[r][:, 0, :], in1=half_sums[r][:, 1, :], op=ALU.add
+            )
+            sums_of[r] = row_sums
+            y_ps = psum_misc.tile([P, ROUND, CHANNELS], F32, tag="misc")
             for a in range(ROUND):
                 for g in range(PASSES):
                     nc.tensor.matmul_mx(
@@ -235,36 +294,87 @@ def tile_causalselfattention_pb_t_kernel(tc, q, k_mix, v_heads, pv_W, pv_b, out)
                         start=(g == 0),
                         stop=(g == PASSES - 1),
                     )
+            y_of[r] = y_ps
+
+        inverses = {}
+
+        def invert_sums(r):
+            inverse = per_round.tile([P, ROUND], F32)
+            nc.vector.reciprocal(out=inverse[:], in_=sums_of[r][:])
+            inverses[r] = inverse
+
+        def normalise(r):
+            b, h = heads[r * ROUND // TILES]
             y_sb = per_round.tile([P, ROUND, CHANNELS], F32)
             nc.vector.tensor_tensor(
                 out=y_sb[:],
-                in0=y_ps[:],
-                in1=inverse[:].unsqueeze(2).to_broadcast([P, ROUND, CHANNELS]),
+                in0=y_of[r][:],
+                in1=inverses[r][:].unsqueeze(2).to_broadcast([P, ROUND, CHANNELS]),
                 op=ALU.mult,
             )
             nc.sync.dma_start(
-                out=out[b, block(r, ROUND * P), block(h, CHANNELS)].rearrange(
+                out=out[b, block(r % (TILES // ROUND), ROUND * P), block(h, CHANNELS)].rearrange(
                     "(a p) d -> p a d", p=P
                 ),
                 in_=y_sb[:],
             )
 
-        flipped = flip_keys_and_queries(0)
-        mixed = None
-        for n in range(len(heads)):
-            kT, qT = flipped
-            e_grouped, row_sums = softmax_round(0, kT, qT)
-            if n == 0:
-                v_grouped = group_values(0)
-                prepare_weights()
-                mixed = mix_values(v_grouped)
-            vm_codes, vm_scales = mixed
-            weighted_sum(n, 0, e_grouped, row_sums, vm_codes, vm_scales)
-            if n + 1 < len(heads):
-                v_grouped = group_values(n + 1)
-                flipped = flip_keys_and_queries(n + 1)
-                mixed = mix_values(v_grouped)
-            if n + AHEAD < len(heads):
-                load_head(n + AHEAD)
-            e_grouped, row_sums = softmax_round(1, kT, qT)
-            weighted_sum(n, 1, e_grouped, row_sums, vm_codes, vm_scales)
+        ctx.enter_context(tc.manual_schedule())
+        flip_rows(0, k_rows, kT_flips)
+        copy_keys(0, nc.vector.tensor_copy)
+        flip_rows(0, q_rows, qT_flips)
+        copy_queries(0, nc.scalar.copy)
+        group_values(0)
+        for n in range(LEAD_S):
+            scores(n)
+        for n in range(LEAD_M):
+            row_maximum(n)
+        for c in range(CHUNKS):
+            for pair in range(PACK // 2):
+                flip_weights(c, pair)
+        for c in range(CHUNKS):
+            quantise_weights(c)
+        quantise_values(0)
+        for n in range(tiles + ROUND + 3):
+            head, j = divmod(n, TILES)
+            inside = n < tiles
+            prepare = inside and head + 1 < len(heads)
+            r, phase = divmod(n - ROUND, ROUND)
+            if inside:
+                exponentials(n)
+            if 0 <= n - 1 < tiles:
+                flip_exponentials(n - 1)
+            if inside and j % ROUND == 0:
+                mix_values(head, j // ROUND)
+            if prepare and j == 1:
+                flip_rows(head + 1, k_rows, kT_flips)
+            if prepare and j == 3:
+                flip_rows(head + 1, q_rows, qT_flips)
+            if 0 <= r < rounds and phase == 2:
+                weighted_sums(r)
+            if n + LEAD_S < tiles:
+                scores(n + LEAD_S)
+            if 0 <= n - 1 < tiles:
+                regroup_exponentials(n - 1, nc.scalar.copy)
+            if prepare and j == 1:
+                copy_keys(head + 1, nc.scalar.copy)
+                group_values(head + 1)
+            if prepare and j == 3:
+                copy_queries(head + 1, nc.scalar.copy)
+            if phase == 3 and r + 1 < rounds:
+                quantise_exponentials(r + 1, 0)
+            if 0 <= r < rounds and phase == 1:
+                quantise_exponentials(r, 1)
+            if n + LEAD_M < tiles:
+                row_maximum(n + LEAD_M)
+            if inside and j % ROUND == 0:
+                add_bias(head, j // ROUND)
+            if inside and j == ROUND + 1:
+                quantise_mixed(head)
+            if prepare and j == TILES - 1:
+                quantise_values(head + 1)
+            if 0 <= r < rounds and phase == 2:
+                invert_sums(r)
+                normalise(r)
+            if j == TILES - 1 and head + AHEAD < len(heads):
+                load_head(head + AHEAD)

@@ -25,8 +25,8 @@ HALVES = TOKENS // BANK
 ROUND = 4
 PAIR = 2
 AHEAD = 3
-LEAD_S = 3
-LEAD_M = 2
+LEAD_S = 2
+LEAD_M = 1
 SCALE = 1.0 / math.sqrt(CHANNELS)
 
 FLOPS = 2 * BATCH * HEADS * (2 * TOKENS * TOKENS * CHANNELS + CHUNKS * CHUNK * CHUNK * CHANNELS)
@@ -44,9 +44,9 @@ def tile_causalselfattention_pb_t_kernel(tc, q, k_mix, v_heads, pv_W, pv_b, out)
         per_head = ctx.enter_context(tc.tile_pool(name="per_head", bufs=2))
         per_tile = ctx.enter_context(tc.tile_pool(name="per_tile", bufs=4))
         per_round = ctx.enter_context(tc.tile_pool(name="per_round", bufs=3))
-        psum_s = ctx.enter_context(tc.psum_pool(name="psum_s", bufs=6))
+        psum_s = ctx.enter_context(tc.psum_pool(name="psum_s", bufs=5))
         psum_e = ctx.enter_context(tc.psum_pool(name="psum_e", bufs=1))
-        psum_misc = ctx.enter_context(tc.psum_pool(name="psum_misc", bufs=1))
+        psum_misc = ctx.enter_context(tc.psum_pool(name="psum_misc", bufs=2))
 
         heads = [(b, h) for b in range(BATCH) for h in range(HEADS)]
         tiles = len(heads) * TILES
@@ -83,8 +83,9 @@ def tile_causalselfattention_pb_t_kernel(tc, q, k_mix, v_heads, pv_W, pv_b, out)
         w_codes = const.tile([P, CHUNKS * PACK * P], U32, align_bytes=64)
         w_scales = const.tile([P, CHUNKS * PACK * P], U8, align_bytes=64)
 
+        w_flips = {}
+
         def flip_weights(c, pair):
-            w_grouped_words = w_grouped[:].bitcast(F32)
             w_flip = psum_misc.tile([P, 2, 2, P], F32, tag="misc")
             for r in range(2):
                 words = (
@@ -92,10 +93,13 @@ def tile_causalselfattention_pb_t_kernel(tc, q, k_mix, v_heads, pv_W, pv_b, out)
                 )
                 for u in range(2):
                     nc.tensor.transpose(w_flip[:, r, u, :], words[:, u, :], ident_f32[:])
+            w_flips[c, pair] = w_flip
+
+        def group_weights(c, pair):
             first = c * PACK + 2 * pair
             nc.vector.tensor_copy(
-                out=w_grouped_words[:, first : first + 2, :, :],
-                in_=w_flip[:].rearrange("p r u m -> p r m u"),
+                out=w_grouped[:].bitcast(F32)[:, first : first + 2, :, :],
+                in_=w_flips[c, pair][:].rearrange("p r u m -> p r m u"),
             )
 
         def quantise_weights(c):
@@ -272,16 +276,18 @@ def tile_causalselfattention_pb_t_kernel(tc, q, k_mix, v_heads, pv_W, pv_b, out)
                 in_=e_grouped[r][:, block(pair, PAIR)].rearrange("p a g m t -> p (a g m t)"),
             )
 
-        sums_of, y_of = {}, {}
+        sums_of, y_of, inverses = {}, {}, {}
 
-        def weighted_sums(r):
-            vm_codes, vm_scales = vm_quantised[r * ROUND // TILES]
-            e_codes, e_scales = e_quantised[r]
+        def add_half_sums(r):
             row_sums = per_round.tile([P, ROUND], F32)
             nc.gpsimd.tensor_tensor(
                 out=row_sums[:], in0=half_sums[r][:, 0, :], in1=half_sums[r][:, 1, :], op=ALU.add
             )
             sums_of[r] = row_sums
+
+        def weighted_sums(r):
+            vm_codes, vm_scales = vm_quantised[r * ROUND // TILES]
+            e_codes, e_scales = e_quantised[r]
             y_ps = psum_misc.tile([P, ROUND, CHANNELS], F32, tag="misc")
             for a in range(ROUND):
                 for g in range(PASSES):
@@ -295,8 +301,6 @@ def tile_causalselfattention_pb_t_kernel(tc, q, k_mix, v_heads, pv_W, pv_b, out)
                         stop=(g == PASSES - 1),
                     )
             y_of[r] = y_ps
-
-        inverses = {}
 
         def invert_sums(r):
             inverse = per_round.tile([P, ROUND], F32)
@@ -329,52 +333,69 @@ def tile_causalselfattention_pb_t_kernel(tc, q, k_mix, v_heads, pv_W, pv_b, out)
             scores(n)
         for n in range(LEAD_M):
             row_maximum(n)
-        for c in range(CHUNKS):
-            for pair in range(PACK // 2):
-                flip_weights(c, pair)
-        for c in range(CHUNKS):
-            quantise_weights(c)
-        quantise_values(0)
-        for n in range(tiles + ROUND + 3):
+        for n in range(tiles + 2 * ROUND):
             head, j = divmod(n, TILES)
             inside = n < tiles
+            first = inside and head == 0
             prepare = inside and head + 1 < len(heads)
-            r, phase = divmod(n - ROUND, ROUND)
+            r, phase = divmod(n, ROUND)
             if inside:
                 exponentials(n)
             if 0 <= n - 1 < tiles:
                 flip_exponentials(n - 1)
-            if inside and j % ROUND == 0:
-                mix_values(head, j // ROUND)
-            if prepare and j == 1:
-                flip_rows(head + 1, k_rows, kT_flips)
-            if prepare and j == 3:
-                flip_rows(head + 1, q_rows, qT_flips)
-            if 0 <= r < rounds and phase == 2:
-                weighted_sums(r)
             if n + LEAD_S < tiles:
                 scores(n + LEAD_S)
+            if n < CHUNKS:
+                for pair in range(PACK // 2):
+                    flip_weights(n, pair)
+            if prepare and j == 0:
+                flip_rows(head + 1, k_rows, kT_flips)
+            if prepare and j == 2:
+                flip_rows(head + 1, q_rows, qT_flips)
+            if first and j in (3, 4):
+                mix_values(0, j - 3)
+            if prepare and j == 5:
+                mix_values(head + 1, 0)
+            if inside and head > 0 and j == 1:
+                mix_values(head, 1)
+            if phase == 3 and 0 <= r - 1 < rounds:
+                weighted_sums(r - 1)
             if 0 <= n - 1 < tiles:
                 regroup_exponentials(n - 1, nc.scalar.copy)
-            if prepare and j == 1:
-                copy_keys(head + 1, nc.scalar.copy)
-                group_values(head + 1)
-            if prepare and j == 3:
+            if prepare and j == 2:
                 copy_queries(head + 1, nc.scalar.copy)
-            if phase == 3 and r + 1 < rounds:
-                quantise_exponentials(r + 1, 0)
-            if 0 <= r < rounds and phase == 1:
-                quantise_exponentials(r, 1)
             if n + LEAD_M < tiles:
                 row_maximum(n + LEAD_M)
-            if inside and j % ROUND == 0:
-                add_bias(head, j // ROUND)
-            if inside and j == ROUND + 1:
+            if 1 <= n <= CHUNKS:
+                for pair in range(PACK // 2):
+                    group_weights(n - 1, pair)
+            if first and j in (4, 5):
+                add_bias(0, j - 4)
+            if prepare and j == 6:
+                add_bias(head + 1, 0)
+            if inside and head > 0 and j == 2:
+                add_bias(head, 1)
+            if prepare and j == 1:
+                copy_keys(head + 1, nc.vector.tensor_copy)
+            if phase == 0 and 0 <= r - 2 < rounds:
+                normalise(r - 2)
+            if 1 <= n <= CHUNKS:
+                quantise_weights(n - 1)
+            if n == 2:
+                quantise_values(0)
+            if phase == 3 and r < rounds:
+                quantise_exponentials(r, 0)
+            if phase == 1 and 0 <= r - 1 < rounds:
+                quantise_exponentials(r - 1, 1)
+            if inside and j == (6 if first else 5):
                 quantise_mixed(head)
-            if prepare and j == TILES - 1:
+            if prepare and j == 3:
                 quantise_values(head + 1)
-            if 0 <= r < rounds and phase == 2:
-                invert_sums(r)
-                normalise(r)
+            if phase == 0 and 0 <= r - 1 < rounds:
+                add_half_sums(r - 1)
+            if phase == 2 and 0 <= r - 1 < rounds:
+                invert_sums(r - 1)
+            if prepare and j == 2:
+                group_values(head + 1)
             if j == TILES - 1 and head + AHEAD < len(heads):
                 load_head(head + AHEAD)

@@ -233,8 +233,8 @@ def tile_causalselfattention_pb_t_kernel(tc, q, k_mix, v_heads, pv_W, pv_b, out)
             e_rows = per_tile.tile([P, TOKENS], BF16)
             for half in range(HALVES):
                 nc.scalar.activation(
-                    out=e_rows[:, block(half, BANK)],
-                    in_=s_halves[n][half][:],
+                    out=e_rows[:, block(half, BANK)].rearrange("p (u w e) -> p u w e", u=2, e=2),
+                    in_=s_halves[n][half][:].rearrange("p (w u e) -> p u w e", u=2, e=2),
                     func=ACT.Exp,
                     bias=shifts[n][:, 0:1],
                     scale=SCALE,
@@ -243,7 +243,7 @@ def tile_causalselfattention_pb_t_kernel(tc, q, k_mix, v_heads, pv_W, pv_b, out)
             e_rows_of[n] = e_rows
 
         def flip_exponentials(n):
-            words = e_rows_of[n][:].bitcast(F32).rearrange("p (g w u) -> p g u w", g=PASSES, u=2)
+            words = e_rows_of[n][:].bitcast(F32).rearrange("p (g u w) -> p g u w", g=PASSES, u=2)
             e_flip = psum_e.tile([P, PASSES, 2, P], F32)
             for g in range(PASSES):
                 for u in range(2):

@@ -11,7 +11,6 @@ U8 = mybir.dt.uint8
 FP8X4 = mybir.dt.float8_e4m3fn_x4
 ALU = mybir.AluOpType
 ACT = mybir.ActivationFunctionType
-AXIS_X = mybir.AxisListType.X
 
 BATCH, HEADS, TOKENS, CHANNELS = 4, 4, 1024, 128
 CHUNKS, CHUNK = 2, 512
@@ -25,8 +24,8 @@ HALVES = TOKENS // BANK
 ROUND = 4
 PAIR = 2
 AHEAD = 3
-LEAD_S = 2
-LEAD_M = 1
+LEAD_S = 3
+LEAD_M = 2
 SCALE = 1.0 / math.sqrt(CHANNELS)
 
 FLOPS = 2 * BATCH * HEADS * (2 * TOKENS * TOKENS * CHANNELS + CHUNKS * CHUNK * CHUNK * CHANNELS)
@@ -44,8 +43,8 @@ def tile_causalselfattention_pb_t_kernel(tc, q, k_mix, v_heads, pv_W, pv_b, out)
         per_head = ctx.enter_context(tc.tile_pool(name="per_head", bufs=2))
         per_tile = ctx.enter_context(tc.tile_pool(name="per_tile", bufs=4))
         per_round = ctx.enter_context(tc.tile_pool(name="per_round", bufs=3))
-        psum_s = ctx.enter_context(tc.psum_pool(name="psum_s", bufs=5))
-        psum_e = ctx.enter_context(tc.psum_pool(name="psum_e", bufs=1))
+        psum_s = ctx.enter_context(tc.psum_pool(name="psum_s", bufs=4))
+        psum_e = ctx.enter_context(tc.psum_pool(name="psum_e", bufs=2))
         psum_misc = ctx.enter_context(tc.psum_pool(name="psum_misc", bufs=2))
 
         heads = [(b, h) for b in range(BATCH) for h in range(HEADS)]
@@ -54,19 +53,37 @@ def tile_causalselfattention_pb_t_kernel(tc, q, k_mix, v_heads, pv_W, pv_b, out)
 
         k_rows, q_rows, v_rows = {}, {}, {}
 
+        def load_values(n):
+            b, h = heads[n]
+            v_in = raw.tile([P, CHUNKS, PACK, CHANNELS], BF16)
+            nc.sync.dma_start(
+                out=v_in[:], in_=v_heads[b, h].rearrange("(c p j) d -> p c j d", c=CHUNKS, j=PACK)
+            )
+            v_rows[n] = v_in
+
         def load_head(n):
             b, h = heads[n]
             k_in = raw.tile([P, TILES, CHANNELS], BF16)
             nc.sync.dma_start(out=k_in[:], in_=k_mix[b, h].rearrange("(i p) d -> p i d", p=P))
             q_in = raw.tile([P, TILES, CHANNELS], BF16)
             nc.sync.dma_start(out=q_in[:], in_=q[b, h].rearrange("(i p) d -> p i d", p=P))
-            v_in = raw.tile([P, CHUNKS, PACK, CHANNELS], BF16)
-            nc.sync.dma_start(
-                out=v_in[:], in_=v_heads[b, h].rearrange("(c p j) d -> p c j d", c=CHUNKS, j=PACK)
-            )
-            k_rows[n], q_rows[n], v_rows[n] = k_in, q_in, v_in
+            k_rows[n], q_rows[n] = k_in, q_in
+            load_values(n)
 
-        load_head(0)
+        k_first = raw.tile([P, TILES, CHANNELS], BF16, tag="k_in")
+        q_first = raw.tile([P, TILES, CHANNELS], BF16, tag="q_in")
+        for rows, source, start, stop in (
+            (k_first, k_mix, 0, TILES // 2),
+            (q_first, q, 0, 1),
+            (k_first, k_mix, TILES // 2, TILES),
+            (q_first, q, 1, TILES),
+        ):
+            nc.sync.dma_start(
+                out=rows[:, start:stop, :],
+                in_=source[0, 0, start * P : stop * P].rearrange("(i p) d -> p i d", p=P),
+            )
+        k_rows[0], q_rows[0] = k_first, q_first
+        load_values(0)
         w_rows = const.tile([P, CHUNKS, PACK, CHUNK], BF16)
         nc.sync.dma_start(out=w_rows[:], in_=pv_W.rearrange("c (p t) n -> p c t n", t=PACK))
         bias = const.tile([P, CHUNKS, PACK], BF16)
@@ -126,6 +143,12 @@ def tile_causalselfattention_pb_t_kernel(tc, q, k_mix, v_heads, pv_W, pv_b, out)
             queries = per_head.tile([P, TOKENS], BF16)
             copy(out=queries[:], in_=qT_flips[n][:])
             qT[n] = queries
+
+        def flip_piece(rows, flipped, start, stop, copy, pool, tag):
+            flip = pool.tile([P, (stop - start) * P], BF16, tag=tag)
+            for i in range(start, stop):
+                nc.tensor.transpose(flip[:, block(i - start, P)], rows[0][:, i, :], ident_bf16[:])
+            copy(out=flipped[:, start * P : stop * P], in_=flip[:])
 
         v_grouped, v_quantised, vm_banks, vm_grouped, vm_quantised = {}, {}, {}, {}, {}
 
@@ -188,8 +211,8 @@ def tile_causalselfattention_pb_t_kernel(tc, q, k_mix, v_heads, pv_W, pv_b, out)
             )
             vm_quantised[n] = (vm_codes, vm_scales)
 
-        s_halves, shifts, e_rows_of, e_flips = {}, {}, {}, {}
-        e_grouped, half_sums, e_quantised = {}, {}, {}
+        s_halves, negated, e_rows_of, e_flips = {}, {}, {}, {}
+        sums_of, e_grouped, e_quantised = {}, {}, {}
 
         def scores(n):
             head, i = divmod(n, TILES)
@@ -205,41 +228,44 @@ def tile_causalselfattention_pb_t_kernel(tc, q, k_mix, v_heads, pv_W, pv_b, out)
                 )
                 s_halves[n].append(s_half)
 
-        def row_maximum(n):
-            highest = per_tile.tile([P, HALVES], F32)
+        def negate_scores(n):
+            neg_s = per_tile.tile([P, HALVES, BANK], F32)
+            lowest = per_tile.tile([P, HALVES], F32)
             for half in range(HALVES):
-                nc.vector.tensor_reduce(
-                    out=highest[:, half : half + 1],
-                    in_=s_halves[n][half][:],
-                    axis=AXIS_X,
-                    op=ALU.max,
+                nc.vector.tensor_scalar(
+                    out=neg_s[:, half, :].rearrange("p (u w e) -> p u w e", u=2, e=2),
+                    in0=s_halves[n][half][:].rearrange("p (w u e) -> p u w e", u=2, e=2),
+                    scalar1=-SCALE,
+                    scalar2=None,
+                    op0=ALU.mult,
+                    op1=ALU.min,
+                    accum_out=lowest[:, half : half + 1],
                 )
             shift = per_tile.tile([P, 1], F32)
             nc.gpsimd.tensor_scalar(
                 out=shift[:],
-                in0=highest[:, 0:1],
-                scalar1=highest[:, 1:2],
-                scalar2=-SCALE,
-                op0=ALU.max,
-                op1=ALU.mult,
+                in0=lowest[:, 0:1],
+                scalar1=lowest[:, 1:2],
+                scalar2=None,
+                op0=ALU.min,
             )
-            shifts[n] = shift
+            negated[n] = (neg_s, shift)
 
         def exponentials(n):
             r, a = divmod(n, ROUND)
             if a == 0:
-                sums = per_round.tile([P, HALVES, ROUND], F32)
-                half_sums[r] = sums
+                sums = per_round.tile([P, ROUND], F32)
+                sums_of[r] = sums
+            neg_s, shift = negated[n]
             e_rows = per_tile.tile([P, TOKENS], BF16)
-            for half in range(HALVES):
-                nc.scalar.activation(
-                    out=e_rows[:, block(half, BANK)].rearrange("p (u w e) -> p u w e", u=2, e=2),
-                    in_=s_halves[n][half][:].rearrange("p (w u e) -> p u w e", u=2, e=2),
-                    func=ACT.Exp,
-                    bias=shifts[n][:, 0:1],
-                    scale=SCALE,
-                    accum_out=half_sums[r][:, half, a : a + 1],
-                )
+            nc.scalar.activation(
+                out=e_rows[:],
+                in_=neg_s[:].rearrange("p h k -> p (h k)"),
+                func=ACT.Exp,
+                bias=shift[:, 0:1],
+                scale=-1.0,
+                accum_out=sums_of[r][:, a : a + 1],
+            )
             e_rows_of[n] = e_rows
 
         def flip_exponentials(n):
@@ -263,36 +289,29 @@ def tile_causalselfattention_pb_t_kernel(tc, q, k_mix, v_heads, pv_W, pv_b, out)
             )
             copy(out=grouped_words, in_=e_flips[n][:].rearrange("p g u m -> p g m u"))
 
-        def quantise_exponentials(r, pair):
-            if pair == 0:
+        def quantise_exponentials(r, start, stop):
+            if start == 0:
                 e_codes = per_round.tile([P, ROUND * PASSES * P], U32, align_bytes=64)
                 e_scales = per_round.tile([P, ROUND * PASSES * P], U8, align_bytes=64)
                 e_quantised[r] = (e_codes, e_scales)
             e_codes, e_scales = e_quantised[r]
-            width = PAIR * PASSES * P
+            columns = slice(start * PASSES * P, stop * PASSES * P)
             nc.vector.quantize_mx(
-                out=e_codes[:, block(pair, width)].bitcast(FP8X4),
-                scales=e_scales[:, block(pair, width)],
-                in_=e_grouped[r][:, block(pair, PAIR)].rearrange("p a g m t -> p (a g m t)"),
+                out=e_codes[:, columns].bitcast(FP8X4),
+                scales=e_scales[:, columns],
+                in_=e_grouped[r][:, start:stop].rearrange("p a g m t -> p (a g m t)"),
             )
 
-        sums_of, y_of, inverses = {}, {}, {}
+        y_of, inverses = {}, {}
 
-        def add_half_sums(r):
-            row_sums = per_round.tile([P, ROUND], F32)
-            nc.gpsimd.tensor_tensor(
-                out=row_sums[:], in0=half_sums[r][:, 0, :], in1=half_sums[r][:, 1, :], op=ALU.add
-            )
-            sums_of[r] = row_sums
-
-        def weighted_sums(r):
+        def weighted_sums(r, start, stop):
             vm_codes, vm_scales = vm_quantised[r * ROUND // TILES]
             e_codes, e_scales = e_quantised[r]
-            y_ps = psum_misc.tile([P, ROUND, CHANNELS], F32, tag="misc")
-            for a in range(ROUND):
+            y_ps = psum_misc.tile([P, stop - start, CHANNELS], F32, tag="misc")
+            for a in range(start, stop):
                 for g in range(PASSES):
                     nc.tensor.matmul_mx(
-                        out=y_ps[:, a, :],
+                        out=y_ps[:, a - start, :],
                         lhsT=e_codes[:, block(a * PASSES + g, P)].bitcast(FP8X4),
                         lhsT_scale=e_scales[:, block(a * PASSES + g, P)],
                         rhs=vm_codes[:, block(g, CHANNELS)].bitcast(FP8X4),
@@ -300,40 +319,48 @@ def tile_causalselfattention_pb_t_kernel(tc, q, k_mix, v_heads, pv_W, pv_b, out)
                         start=(g == 0),
                         stop=(g == PASSES - 1),
                     )
-            y_of[r] = y_ps
+            y_of[r, start] = y_ps
 
         def invert_sums(r):
             inverse = per_round.tile([P, ROUND], F32)
             nc.vector.reciprocal(out=inverse[:], in_=sums_of[r][:])
             inverses[r] = inverse
 
-        def normalise(r):
+        def normalise(r, start, stop):
             b, h = heads[r * ROUND // TILES]
-            y_sb = per_round.tile([P, ROUND, CHANNELS], F32)
+            count = stop - start
+            y_sb = per_round.tile([P, count, CHANNELS], F32)
             nc.vector.tensor_tensor(
                 out=y_sb[:],
-                in0=y_of[r][:],
-                in1=inverses[r][:].unsqueeze(2).to_broadcast([P, ROUND, CHANNELS]),
+                in0=y_of[r, start][:],
+                in1=inverses[r][:, start:stop].unsqueeze(2).to_broadcast([P, count, CHANNELS]),
                 op=ALU.mult,
             )
+            first = (r % (TILES // ROUND)) * ROUND + start
             nc.sync.dma_start(
-                out=out[b, block(r % (TILES // ROUND), ROUND * P), block(h, CHANNELS)].rearrange(
+                out=out[b, first * P : (first + count) * P, block(h, CHANNELS)].rearrange(
                     "(a p) d -> p a d", p=P
                 ),
                 in_=y_sb[:],
             )
 
         ctx.enter_context(tc.manual_schedule())
-        flip_rows(0, k_rows, kT_flips)
-        copy_keys(0, nc.vector.tensor_copy)
-        flip_rows(0, q_rows, qT_flips)
-        copy_queries(0, nc.scalar.copy)
+        half = TILES // 2
+        keys = per_head.tile([P, TOKENS], BF16)
+        queries = per_head.tile([P, TOKENS], BF16)
+        kT[0], qT[0] = keys, queries
+        flip_piece(k_rows, keys, 0, half, nc.vector.tensor_copy, psum_misc, "misc")
+        flip_piece(q_rows, queries, 0, 1, nc.scalar.copy, psum_misc, "misc")
+        flip_piece(k_rows, keys, half, TILES, nc.vector.tensor_copy, psum_e, "e_flip")
+        scores(0)
+        flip_piece(q_rows, queries, 1, TILES, nc.scalar.copy, psum_misc, "misc")
+        negate_scores(0)
         group_values(0)
-        for n in range(LEAD_S):
+        for n in range(1, LEAD_S):
             scores(n)
-        for n in range(LEAD_M):
-            row_maximum(n)
-        for n in range(tiles + 2 * ROUND):
+        for n in range(1, LEAD_M):
+            negate_scores(n)
+        for n in range(tiles + 1):
             head, j = divmod(n, TILES)
             inside = n < tiles
             first = inside and head == 0
@@ -341,61 +368,68 @@ def tile_causalselfattention_pb_t_kernel(tc, q, k_mix, v_heads, pv_W, pv_b, out)
             r, phase = divmod(n, ROUND)
             if inside:
                 exponentials(n)
-            if 0 <= n - 1 < tiles:
+            if n > 0:
                 flip_exponentials(n - 1)
             if n + LEAD_S < tiles:
                 scores(n + LEAD_S)
             if n < CHUNKS:
                 for pair in range(PACK // 2):
                     flip_weights(n, pair)
-            if prepare and j == 0:
-                flip_rows(head + 1, k_rows, kT_flips)
             if prepare and j == 2:
+                flip_rows(head + 1, k_rows, kT_flips)
+            if prepare and j == 4:
                 flip_rows(head + 1, q_rows, qT_flips)
-            if first and j in (3, 4):
-                mix_values(0, j - 3)
-            if prepare and j == 5:
+            if first and j in (4, 5):
+                mix_values(0, j - 4)
+            if prepare and j == 6:
                 mix_values(head + 1, 0)
-            if inside and head > 0 and j == 1:
+            if inside and head > 0 and j == 2:
                 mix_values(head, 1)
-            if phase == 3 and 0 <= r - 1 < rounds:
-                weighted_sums(r - 1)
-            if 0 <= n - 1 < tiles:
+            if phase == 0 and r >= 2:
+                weighted_sums(r - 2, 0, ROUND)
+            if n > 0:
                 regroup_exponentials(n - 1, nc.scalar.copy)
             if prepare and j == 2:
+                copy_keys(head + 1, nc.scalar.copy)
+            if prepare and j == 4:
                 copy_queries(head + 1, nc.scalar.copy)
             if n + LEAD_M < tiles:
-                row_maximum(n + LEAD_M)
+                negate_scores(n + LEAD_M)
             if 1 <= n <= CHUNKS:
                 for pair in range(PACK // 2):
                     group_weights(n - 1, pair)
-            if first and j in (4, 5):
-                add_bias(0, j - 4)
-            if prepare and j == 6:
+            if first and j in (5, 6):
+                add_bias(0, j - 5)
+            if prepare and j == 7:
                 add_bias(head + 1, 0)
-            if inside and head > 0 and j == 2:
+            if inside and head > 0 and j == 3:
                 add_bias(head, 1)
-            if prepare and j == 1:
-                copy_keys(head + 1, nc.vector.tensor_copy)
-            if phase == 0 and 0 <= r - 2 < rounds:
-                normalise(r - 2)
-            if 1 <= n <= CHUNKS:
-                quantise_weights(n - 1)
-            if n == 2:
+            if phase == 1 and r >= 2:
+                normalise(r - 2, 0, ROUND)
+            if 2 <= n < 2 + CHUNKS:
+                quantise_weights(n - 2)
+            if n == 3:
                 quantise_values(0)
-            if phase == 3 and r < rounds:
-                quantise_exponentials(r, 0)
-            if phase == 1 and 0 <= r - 1 < rounds:
-                quantise_exponentials(r - 1, 1)
-            if inside and j == (6 if first else 5):
+            if phase == 0 and r >= 1:
+                quantise_exponentials(r - 1, 0, PAIR)
+            if phase == 2 and r >= 1:
+                quantise_exponentials(r - 1, PAIR, ROUND)
+            if inside and j == (7 if first else 5):
                 quantise_mixed(head)
-            if prepare and j == 3:
+            if prepare and j == 4:
                 quantise_values(head + 1)
-            if phase == 0 and 0 <= r - 1 < rounds:
-                add_half_sums(r - 1)
-            if phase == 2 and 0 <= r - 1 < rounds:
+            if phase == 3 and r >= 1:
                 invert_sums(r - 1)
-            if prepare and j == 2:
+            if prepare and j == 3:
                 group_values(head + 1)
             if j == TILES - 1 and head + AHEAD < len(heads):
                 load_head(head + AHEAD)
+        last = rounds - 1
+        normalise(last - 1, 0, ROUND)
+        invert_sums(last)
+        quantise_exponentials(last, PAIR, ROUND - 1)
+        weighted_sums(last, 0, ROUND - 1)
+        quantise_exponentials(last, ROUND - 1, ROUND)
+        weighted_sums(last, ROUND - 1, ROUND)
+        normalise(last, 0, ROUND - 1)
+        normalise(last, ROUND - 1, ROUND)

@@ -190,13 +190,21 @@ def tile_causalselfattention_pb_t_kernel(tc, q, k_mix, v_heads, pv_W, pv_b, out)
                 )
             vm_banks[n, c] = vm_ps
 
+        vm_copies = {}
+
+        def copy_mixed(n, c):
+            vm_rows = per_head.tile([P, PACK, CHANNELS], F32)
+            nc.scalar.copy(out=vm_rows[:], in_=vm_banks[n, c][:])
+            vm_copies[n, c] = vm_rows
+
         def add_bias(n, c):
             if c == 0:
                 grouped = per_head.tile([P, CHUNKS, CHANNELS, PACK], BF16, align_bytes=64)
                 vm_grouped[n] = grouped
-            nc.vector.tensor_tensor(
+            engine = nc.gpsimd if (n, c) in vm_copies else nc.vector
+            engine.tensor_tensor(
                 out=vm_grouped[n][:, c],
-                in0=vm_banks[n, c][:].rearrange("p t d -> p d t"),
+                in0=(vm_copies if (n, c) in vm_copies else vm_banks)[n, c][:].rearrange("p t d -> p d t"),
                 in1=bias[:, c, :].unsqueeze(1).to_broadcast([P, CHANNELS, PACK]),
                 op=ALU.add,
             )
@@ -252,10 +260,10 @@ def tile_causalselfattention_pb_t_kernel(tc, q, k_mix, v_heads, pv_W, pv_b, out)
             negated[n] = (neg_s, shift)
 
         def exponentials(n):
-            r, a = divmod(n, ROUND)
-            if a == 0:
-                sums = per_round.tile([P, ROUND], F32)
-                sums_of[r] = sums
+            head, i = divmod(n, TILES)
+            if i == 0:
+                sums = per_head.tile([P, TILES], F32)
+                sums_of[head] = sums
             neg_s, shift = negated[n]
             e_rows = per_tile.tile([P, TOKENS], BF16)
             nc.scalar.activation(
@@ -264,7 +272,7 @@ def tile_causalselfattention_pb_t_kernel(tc, q, k_mix, v_heads, pv_W, pv_b, out)
                 func=ACT.Exp,
                 bias=shift[:, 0:1],
                 scale=-1.0,
-                accum_out=sums_of[r][:, a : a + 1],
+                accum_out=sums_of[head][:, i : i + 1],
             )
             e_rows_of[n] = e_rows
 
@@ -321,22 +329,24 @@ def tile_causalselfattention_pb_t_kernel(tc, q, k_mix, v_heads, pv_W, pv_b, out)
                     )
             y_of[r, start] = y_ps
 
-        def invert_sums(r):
-            inverse = per_round.tile([P, ROUND], F32)
-            nc.vector.reciprocal(out=inverse[:], in_=sums_of[r][:])
-            inverses[r] = inverse
+        def invert_sums(n):
+            inverse = per_head.tile([P, TILES], F32)
+            nc.vector.reciprocal(out=inverse[:], in_=sums_of[n][:])
+            inverses[n] = inverse
 
         def normalise(r, start, stop):
-            b, h = heads[r * ROUND // TILES]
+            head, first = divmod(r * ROUND + start, TILES)
+            b, h = heads[head]
             count = stop - start
             y_sb = per_round.tile([P, count, CHANNELS], F32)
             nc.vector.tensor_tensor(
                 out=y_sb[:],
                 in0=y_of[r, start][:],
-                in1=inverses[r][:, start:stop].unsqueeze(2).to_broadcast([P, count, CHANNELS]),
+                in1=inverses[head][:, first : first + count]
+                .unsqueeze(2)
+                .to_broadcast([P, count, CHANNELS]),
                 op=ALU.mult,
             )
-            first = (r % (TILES // ROUND)) * ROUND + start
             nc.sync.dma_start(
                 out=out[b, first * P : (first + count) * P, block(h, CHANNELS)].rearrange(
                     "(a p) d -> p a d", p=P
@@ -393,6 +403,12 @@ def tile_causalselfattention_pb_t_kernel(tc, q, k_mix, v_heads, pv_W, pv_b, out)
                 copy_keys(head + 1, nc.scalar.copy)
             if prepare and j == 4:
                 copy_queries(head + 1, nc.scalar.copy)
+            if first and j == 4:
+                copy_mixed(0, 0)
+            if prepare and j == 6:
+                copy_mixed(head + 1, 0)
+            if j == 1 and head > 0:
+                invert_sums(head - 1)
             if n + LEAD_M < tiles:
                 negate_scores(n + LEAD_M)
             if 1 <= n <= CHUNKS:
@@ -414,19 +430,17 @@ def tile_causalselfattention_pb_t_kernel(tc, q, k_mix, v_heads, pv_W, pv_b, out)
                 quantise_exponentials(r - 1, 0, PAIR)
             if phase == 2 and r >= 1:
                 quantise_exponentials(r - 1, PAIR, ROUND)
-            if inside and j == (7 if first else 5):
+            if inside and j == 7:
                 quantise_mixed(head)
             if prepare and j == 4:
                 quantise_values(head + 1)
-            if phase == 3 and r >= 1:
-                invert_sums(r - 1)
             if prepare and j == 3:
                 group_values(head + 1)
             if j == TILES - 1 and head + AHEAD < len(heads):
                 load_head(head + AHEAD)
         last = rounds - 1
+        invert_sums(len(heads) - 1)
         normalise(last - 1, 0, ROUND)
-        invert_sums(last)
         quantise_exponentials(last, PAIR, ROUND - 1)
         weighted_sums(last, 0, ROUND - 1)
         quantise_exponentials(last, ROUND - 1, ROUND)

@@ -134,10 +134,11 @@ def tile_causalselfattention_pb_t_kernel(tc, q, k_mix, v_heads, pv_W, pv_b, out)
                 nc.tensor.transpose(flip[:, block(i, P)], rows[n][:, i, :], ident_bf16[:])
             flips[n] = flip
 
-        def copy_keys(n, copy):
-            keys = per_head.tile([P, TOKENS], BF16)
-            copy(out=keys[:], in_=kT_flips[n][:])
-            kT[n] = keys
+        def copy_keys(n, half, copy):
+            if half == 0:
+                keys = per_head.tile([P, TOKENS], BF16)
+                kT[n] = keys
+            copy(out=kT[n][:, block(half, BANK)], in_=kT_flips[n][:, block(half, BANK)])
 
         def copy_queries(n, copy):
             queries = per_head.tile([P, TOKENS], BF16)
@@ -400,7 +401,7 @@ def tile_causalselfattention_pb_t_kernel(tc, q, k_mix, v_heads, pv_W, pv_b, out)
             if n > 0:
                 regroup_exponentials(n - 1, nc.scalar.copy)
             if prepare and j == 2:
-                copy_keys(head + 1, nc.scalar.copy)
+                copy_keys(head + 1, 0, nc.scalar.copy)
             if prepare and j == 4:
                 copy_queries(head + 1, nc.scalar.copy)
             if first and j == 4:
@@ -418,6 +419,8 @@ def tile_causalselfattention_pb_t_kernel(tc, q, k_mix, v_heads, pv_W, pv_b, out)
                 add_bias(0, j - 5)
             if prepare and j == 7:
                 add_bias(head + 1, 0)
+            if prepare and j == 3:
+                copy_keys(head + 1, 1, nc.vector.tensor_copy)
             if inside and head > 0 and j == 3:
                 add_bias(head, 1)
             if phase == 1 and r >= 2:
@@ -426,10 +429,8 @@ def tile_causalselfattention_pb_t_kernel(tc, q, k_mix, v_heads, pv_W, pv_b, out)
                 quantise_weights(n - 2)
             if n == 3:
                 quantise_values(0)
-            if phase == 0 and r >= 1:
-                quantise_exponentials(r - 1, 0, PAIR)
             if phase == 2 and r >= 1:
-                quantise_exponentials(r - 1, PAIR, ROUND)
+                quantise_exponentials(r - 1, 0, ROUND)
             if inside and j == 7:
                 quantise_mixed(head)
             if prepare and j == 4:
@@ -439,6 +440,7 @@ def tile_causalselfattention_pb_t_kernel(tc, q, k_mix, v_heads, pv_W, pv_b, out)
             if j == TILES - 1 and head + AHEAD < len(heads):
                 load_head(head + AHEAD)
         last = rounds - 1
+        quantise_exponentials(last, 0, PAIR)
         invert_sums(len(heads) - 1)
         normalise(last - 1, 0, ROUND)
         quantise_exponentials(last, PAIR, ROUND - 1)

@@ -24,8 +24,10 @@ HALVES = TOKENS // BANK
 ROUND = 4
 PAIR = 2
 AHEAD = 3
+BIAS_PITCH = 16
 LEAD_S = 3
 LEAD_M = 2
+LAST_ON_VECTOR = 3
 SCALE = 1.0 / math.sqrt(CHANNELS)
 
 FLOPS = 2 * BATCH * HEADS * (2 * TOKENS * TOKENS * CHANNELS + CHUNKS * CHUNK * CHUNK * CHANNELS)
@@ -85,9 +87,17 @@ def tile_causalselfattention_pb_t_kernel(tc, q, k_mix, v_heads, pv_W, pv_b, out)
         k_rows[0], q_rows[0] = k_first, q_first
         load_values(0)
         w_rows = const.tile([P, CHUNKS, PACK, CHUNK], BF16)
-        nc.sync.dma_start(out=w_rows[:], in_=pv_W.rearrange("c (p t) n -> p c t n", t=PACK))
-        bias = const.tile([P, CHUNKS, PACK], BF16)
-        nc.sync.dma_start(out=bias[:], in_=pv_b.rearrange("c (p t) -> p c t", t=PACK))
+        bias = const.tile([P, CHUNKS, BIAS_PITCH], BF16)
+        for c in range(CHUNKS):
+            nc.sync.dma_start(
+                out=w_rows[:, c].rearrange("p (u e) n -> p u e n", e=2),
+                in_=pv_W[c].rearrange("(u p e) n -> p u e n", u=2, e=2),
+            )
+        for c in range(CHUNKS):
+            nc.sync.dma_start(
+                out=bias[:, c, 0:PACK].rearrange("p (u e) -> p u e", e=2),
+                in_=pv_b[c].rearrange("(u p e) -> p u e", u=2, e=2),
+            )
         for n in range(1, AHEAD):
             load_head(n)
 
@@ -206,7 +216,7 @@ def tile_causalselfattention_pb_t_kernel(tc, q, k_mix, v_heads, pv_W, pv_b, out)
             engine.tensor_tensor(
                 out=vm_grouped[n][:, c],
                 in0=(vm_copies if (n, c) in vm_copies else vm_banks)[n, c][:].rearrange("p t d -> p d t"),
-                in1=bias[:, c, :].unsqueeze(1).to_broadcast([P, CHANNELS, PACK]),
+                in1=bias[:, c, 0:PACK].unsqueeze(1).to_broadcast([P, CHANNELS, PACK]),
                 op=ALU.add,
             )
 
@@ -242,8 +252,8 @@ def tile_causalselfattention_pb_t_kernel(tc, q, k_mix, v_heads, pv_W, pv_b, out)
             lowest = per_tile.tile([P, HALVES], F32)
             for half in range(HALVES):
                 nc.vector.tensor_scalar(
-                    out=neg_s[:, half, :].rearrange("p (u w e) -> p u w e", u=2, e=2),
-                    in0=s_halves[n][half][:].rearrange("p (w u e) -> p u w e", u=2, e=2),
+                    out=neg_s[:, half, :],
+                    in0=s_halves[n][half][:],
                     scalar1=-SCALE,
                     scalar2=None,
                     op0=ALU.mult,
@@ -398,7 +408,7 @@ def tile_causalselfattention_pb_t_kernel(tc, q, k_mix, v_heads, pv_W, pv_b, out)
                 mix_values(head, 1)
             if phase == 0 and r >= 2:
                 weighted_sums(r - 2, 0, ROUND)
-            if n > 0:
+            if 0 < n <= tiles - LAST_ON_VECTOR:
                 regroup_exponentials(n - 1, nc.scalar.copy)
             if prepare and j == 2:
                 copy_keys(head + 1, 0, nc.scalar.copy)
@@ -412,6 +422,8 @@ def tile_causalselfattention_pb_t_kernel(tc, q, k_mix, v_heads, pv_W, pv_b, out)
                 invert_sums(head - 1)
             if n + LEAD_M < tiles:
                 negate_scores(n + LEAD_M)
+            if n > tiles - LAST_ON_VECTOR:
+                regroup_exponentials(n - 1, nc.vector.tensor_copy)
             if 1 <= n <= CHUNKS:
                 for pair in range(PACK // 2):
                     group_weights(n - 1, pair)

import math
from contextlib import ExitStack

import concourse.mybir as mybir
from concourse.masks import make_identity

BF16 = mybir.dt.bfloat16
F32 = mybir.dt.float32
U32 = mybir.dt.uint32
U8 = mybir.dt.uint8
FP8X4 = mybir.dt.float8_e4m3fn_x4
ALU = mybir.AluOpType
ACT = mybir.ActivationFunctionType

BATCH, HEADS, TOKENS, CHANNELS = 4, 4, 1024, 128
CHUNKS, CHUNK = 2, 512
P = 128
PACK = 4
K_PASS = P * PACK
PASSES = TOKENS // K_PASS
TILES = TOKENS // P
BANK = 512
HALVES = TOKENS // BANK
ROUND = 4
PAIR = 2
AHEAD = 3
BIAS_PITCH = 16
LEAD_S = 3
LEAD_M = 2
LAST_ON_VECTOR = 3
SCALE = 1.0 / math.sqrt(CHANNELS)

FLOPS = 2 * BATCH * HEADS * (2 * TOKENS * TOKENS * CHANNELS + CHUNKS * CHUNK * CHUNK * CHANNELS)


def block(index, width):
    return slice(index * width, (index + 1) * width)


def tile_causalselfattention_pb_t_kernel(tc, q, k_mix, v_heads, pv_W, pv_b, out):
    nc = tc.nc
    with ExitStack() as ctx:
        const = ctx.enter_context(tc.tile_pool(name="const", bufs=1))
        raw = ctx.enter_context(tc.tile_pool(name="raw", bufs=AHEAD))
        per_head = ctx.enter_context(tc.tile_pool(name="per_head", bufs=2))
        per_tile = ctx.enter_context(tc.tile_pool(name="per_tile", bufs=4))
        per_round = ctx.enter_context(tc.tile_pool(name="per_round", bufs=3))
        psum_s = ctx.enter_context(tc.psum_pool(name="psum_s", bufs=4))
        psum_e = ctx.enter_context(tc.psum_pool(name="psum_e", bufs=2))
        psum_misc = ctx.enter_context(tc.psum_pool(name="psum_misc", bufs=2))

        heads = [(b, h) for b in range(BATCH) for h in range(HEADS)]
        tiles = len(heads) * TILES
        rounds = tiles // ROUND

        k_rows, q_rows, v_rows = {}, {}, {}

        def load_values(n):
            b, h = heads[n]
            v_in = raw.tile([P, CHUNKS, PACK, CHANNELS], BF16)
            nc.sync.dma_start(
                out=v_in[:], in_=v_heads[b, h].rearrange("(c p j) d -> p c j d", c=CHUNKS, j=PACK)
            )
            v_rows[n] = v_in

        def load_head(n):
            b, h = heads[n]
            k_in = raw.tile([P, TILES, CHANNELS], BF16)
            nc.sync.dma_start(out=k_in[:], in_=k_mix[b, h].rearrange("(i p) d -> p i d", p=P))
            q_in = raw.tile([P, TILES, CHANNELS], BF16)
            nc.sync.dma_start(out=q_in[:], in_=q[b, h].rearrange("(i p) d -> p i d", p=P))
            k_rows[n], q_rows[n] = k_in, q_in
            load_values(n)

        k_first = raw.tile([P, TILES, CHANNELS], BF16, tag="k_in")
        q_first = raw.tile([P, TILES, CHANNELS], BF16, tag="q_in")
        for rows, source, start, stop in (
            (k_first, k_mix, 0, TILES // 2),
            (q_first, q, 0, 1),
            (k_first, k_mix, TILES // 2, TILES),
            (q_first, q, 1, TILES),
        ):
            nc.sync.dma_start(
                out=rows[:, start:stop, :],
                in_=source[0, 0, start * P : stop * P].rearrange("(i p) d -> p i d", p=P),
            )
        k_rows[0], q_rows[0] = k_first, q_first
        load_values(0)
        w_rows = const.tile([P, CHUNKS, PACK, CHUNK], BF16)
        bias = const.tile([P, CHUNKS, BIAS_PITCH], BF16)
        for c in range(CHUNKS):
            nc.sync.dma_start(
                out=w_rows[:, c].rearrange("p (u e) n -> p u e n", e=2),
                in_=pv_W[c].rearrange("(u p e) n -> p u e n", u=2, e=2),
            )
        for c in range(CHUNKS):
            nc.sync.dma_start(
                out=bias[:, c, 0:PACK].rearrange("p (u e) -> p u e", e=2),
                in_=pv_b[c].rearrange("(u p e) -> p u e", u=2, e=2),
            )
        for n in range(1, AHEAD):
            load_head(n)

        ident_bf16 = const.tile([P, P], BF16)
        make_identity(nc, ident_bf16[:])
        ident_f32 = const.tile([P, P], F32)
        make_identity(nc, ident_f32[:])

        w_grouped = const.tile([P, CHUNKS * PACK, P, PACK], BF16, align_bytes=64)
        w_codes = const.tile([P, CHUNKS * PACK * P], U32, align_bytes=64)
        w_scales = const.tile([P, CHUNKS * PACK * P], U8, align_bytes=64)

        w_flips = {}

        def flip_weights(c, pair):
            w_flip = psum_misc.tile([P, 2, 2, P], F32, tag="misc")
            for r in range(2):
                words = (
                    w_rows[:, c, 2 * pair + r, :].bitcast(F32).rearrange("p (w u) -> p u w", u=2)
                )
                for u in range(2):
                    nc.tensor.transpose(w_flip[:, r, u, :], words[:, u, :], ident_f32[:])
            w_flips[c, pair] = w_flip

        def group_weights(c, pair):
            first = c * PACK + 2 * pair
            nc.vector.tensor_copy(
                out=w_grouped[:].bitcast(F32)[:, first : first + 2, :, :],
                in_=w_flips[c, pair][:].rearrange("p r u m -> p r m u"),
            )

        def quantise_weights(c):
            nc.vector.quantize_mx(
                out=w_codes[:, block(c, PACK * P)].bitcast(FP8X4),
                scales=w_scales[:, block(c, PACK * P)],
                in_=w_grouped[:, block(c, PACK)].rearrange("p a m t -> p (a m t)"),
            )

        kT, qT, kT_flips, qT_flips = {}, {}, {}, {}

        def flip_rows(n, rows, flips):
            flip = psum_misc.tile([P, TOKENS], BF16, tag="misc")
            for i in range(TILES):
                nc.tensor.transpose(flip[:, block(i, P)], rows[n][:, i, :], ident_bf16[:])
            flips[n] = flip

        def copy_keys(n, half, copy):
            if half == 0:
                keys = per_head.tile([P, TOKENS], BF16)
                kT[n] = keys
            copy(out=kT[n][:, block(half, BANK)], in_=kT_flips[n][:, block(half, BANK)])

        def copy_queries(n, copy):
            queries = per_head.tile([P, TOKENS], BF16)
            copy(out=queries[:], in_=qT_flips[n][:])
            qT[n] = queries

        def flip_piece(rows, flipped, start, stop, copy, pool, tag):
            flip = pool.tile([P, (stop - start) * P], BF16, tag=tag)
            for i in range(start, stop):
                nc.tensor.transpose(flip[:, block(i - start, P)], rows[0][:, i, :], ident_bf16[:])
            copy(out=flipped[:, start * P : stop * P], in_=flip[:])

        v_grouped, v_quantised, vm_banks, vm_grouped, vm_quantised = {}, {}, {}, {}, {}

        def group_values(n):
            grouped = per_head.tile([P, CHUNKS, CHANNELS, PACK], BF16, align_bytes=64)
            for c in range(CHUNKS):
                nc.gpsimd.tensor_scalar(
                    out=grouped[:, c],
                    in0=v_rows[n][:, c].rearrange("p j d -> p d j"),
                    scalar1=1.0,
                    scalar2=0.0,
                    op0=ALU.mult,
                    op1=ALU.add,
                )
            v_grouped[n] = grouped

        def quantise_values(n):
            v_codes = per_head.tile([P, CHUNKS * CHANNELS], U32, align_bytes=64)
            v_scales = per_head.tile([P, CHUNKS * CHANNELS], U8, align_bytes=64)
            nc.vector.quantize_mx(
                out=v_codes[:].bitcast(FP8X4),
                scales=v_scales[:],
                in_=v_grouped[n][:].rearrange("p c d j -> p (c d j)"),
            )
            v_quantised[n] = (v_codes, v_scales)

        def mix_values(n, c):
            v_codes, v_scales = v_quantised[n]
            vm_ps = psum_misc.tile([P, PACK, CHANNELS], F32, tag="misc")
            for t in range(PACK):
                nc.tensor.matmul_mx(
                    out=vm_ps[:, t, :],
                    lhsT=w_codes[:, block(c * PACK + t, P)].bitcast(FP8X4),
                    lhsT_scale=w_scales[:, block(c * PACK + t, P)],
                    rhs=v_codes[:, block(c, CHANNELS)].bitcast(FP8X4),
                    rhs_scale=v_scales[:, block(c, CHANNELS)],
                    start=True,
                    stop=True,
                )
            vm_banks[n, c] = vm_ps

        vm_copies = {}

        def copy_mixed(n, c):
            vm_rows = per_head.tile([P, PACK, CHANNELS], F32)
            nc.scalar.copy(out=vm_rows[:], in_=vm_banks[n, c][:])
            vm_copies[n, c] = vm_rows

        def add_bias(n, c):
            if c == 0:
                grouped = per_head.tile([P, CHUNKS, CHANNELS, PACK], BF16, align_bytes=64)
                vm_grouped[n] = grouped
            engine = nc.gpsimd if (n, c) in vm_copies else nc.vector
            engine.tensor_tensor(
                out=vm_grouped[n][:, c],
                in0=(vm_copies if (n, c) in vm_copies else vm_banks)[n, c][:].rearrange("p t d -> p d t"),
                in1=bias[:, c, 0:PACK].unsqueeze(1).to_broadcast([P, CHANNELS, PACK]),
                op=ALU.add,
            )

        def quantise_mixed(n):
            vm_codes = per_head.tile([P, PASSES * CHANNELS], U32, align_bytes=64)
            vm_scales = per_head.tile([P, PASSES * CHANNELS], U8, align_bytes=64)
            nc.vector.quantize_mx(
                out=vm_codes[:].bitcast(FP8X4),
                scales=vm_scales[:],
                in_=vm_grouped[n][:].rearrange("p c d t -> p (c d t)"),
            )
            vm_quantised[n] = (vm_codes, vm_scales)

        s_halves, negated, e_rows_of, e_flips = {}, {}, {}, {}
        sums_of, e_grouped, e_quantised = {}, {}, {}

        def scores(n):
            head, i = divmod(n, TILES)
            s_halves[n] = []
            for half in range(HALVES):
                s_half = psum_s.tile([P, BANK], F32)
                nc.tensor.matmul(
                    out=s_half[:],
                    lhsT=qT[head][:, block(i, P)],
                    rhs=kT[head][:, block(half, BANK)],
                    start=True,
                    stop=True,
                )
                s_halves[n].append(s_half)

        def negate_scores(n):
            neg_s = per_tile.tile([P, HALVES, BANK], F32)
            lowest = per_tile.tile([P, HALVES], F32)
            for half in range(HALVES):
                nc.vector.tensor_scalar(
                    out=neg_s[:, half, :],
                    in0=s_halves[n][half][:],
                    scalar1=-SCALE,
                    scalar2=None,
                    op0=ALU.mult,
                    op1=ALU.min,
                    accum_out=lowest[:, half : half + 1],
                )
            shift = per_tile.tile([P, 1], F32)
            nc.gpsimd.tensor_scalar(
                out=shift[:],
                in0=lowest[:, 0:1],
                scalar1=lowest[:, 1:2],
                scalar2=None,
                op0=ALU.min,
            )
            negated[n] = (neg_s, shift)

        def exponentials(n):
            head, i = divmod(n, TILES)
            if i == 0:
                sums = per_head.tile([P, TILES], F32)
                sums_of[head] = sums
            neg_s, shift = negated[n]
            e_rows = per_tile.tile([P, TOKENS], BF16)
            nc.scalar.activation(
                out=e_rows[:],
                in_=neg_s[:].rearrange("p h k -> p (h k)"),
                func=ACT.Exp,
                bias=shift[:, 0:1],
                scale=-1.0,
                accum_out=sums_of[head][:, i : i + 1],
            )
            e_rows_of[n] = e_rows

        def flip_exponentials(n):
            words = e_rows_of[n][:].bitcast(F32).rearrange("p (g u w) -> p g u w", g=PASSES, u=2)
            e_flip = psum_e.tile([P, PASSES, 2, P], F32)
            for g in range(PASSES):
                for u in range(2):
                    nc.tensor.transpose(e_flip[:, g, u, :], words[:, g, u, :], ident_f32[:])
            e_flips[n] = e_flip

        def regroup_exponentials(n, copy):
            r, a = divmod(n, ROUND)
            if a == 0:
                grouped = per_round.tile([P, ROUND, PASSES, P, PACK], BF16, align_bytes=64)
                e_grouped[r] = grouped
            grouped_words = (
                e_grouped[r][:, a]
                .rearrange("p g m t -> p (g m t)")
                .bitcast(F32)
                .rearrange("p (g m u) -> p g m u", g=PASSES, u=2)
            )
            copy(out=grouped_words, in_=e_flips[n][:].rearrange("p g u m -> p g m u"))

        def quantise_exponentials(r, start, stop):
            if start == 0:
                e_codes = per_round.tile([P, ROUND * PASSES * P], U32, align_bytes=64)
                e_scales = per_round.tile([P, ROUND * PASSES * P], U8, align_bytes=64)
                e_quantised[r] = (e_codes, e_scales)
            e_codes, e_scales = e_quantised[r]
            columns = slice(start * PASSES * P, stop * PASSES * P)
            nc.vector.quantize_mx(
                out=e_codes[:, columns].bitcast(FP8X4),
                scales=e_scales[:, columns],
                in_=e_grouped[r][:, start:stop].rearrange("p a g m t -> p (a g m t)"),
            )

        y_of, inverses = {}, {}

        def weighted_sums(r, start, stop):
            vm_codes, vm_scales = vm_quantised[r * ROUND // TILES]
            e_codes, e_scales = e_quantised[r]
            y_ps = psum_misc.tile([P, stop - start, CHANNELS], F32, tag="misc")
            for a in range(start, stop):
                for g in range(PASSES):
                    nc.tensor.matmul_mx(
                        out=y_ps[:, a - start, :],
                        lhsT=e_codes[:, block(a * PASSES + g, P)].bitcast(FP8X4),
                        lhsT_scale=e_scales[:, block(a * PASSES + g, P)],
                        rhs=vm_codes[:, block(g, CHANNELS)].bitcast(FP8X4),
                        rhs_scale=vm_scales[:, block(g, CHANNELS)],
                        start=(g == 0),
                        stop=(g == PASSES - 1),
                    )
            y_of[r, start] = y_ps

        def invert_sums(n):
            inverse = per_head.tile([P, TILES], F32)
            nc.vector.reciprocal(out=inverse[:], in_=sums_of[n][:])
            inverses[n] = inverse

        def normalise(r, start, stop):
            head, first = divmod(r * ROUND + start, TILES)
            b, h = heads[head]
            count = stop - start
            y_sb = per_round.tile([P, count, CHANNELS], F32)
            nc.vector.tensor_tensor(
                out=y_sb[:],
                in0=y_of[r, start][:],
                in1=inverses[head][:, first : first + count]
                .unsqueeze(2)
                .to_broadcast([P, count, CHANNELS]),
                op=ALU.mult,
            )
            nc.sync.dma_start(
                out=out[b, first * P : (first + count) * P, block(h, CHANNELS)].rearrange(
                    "(a p) d -> p a d", p=P
                ),
                in_=y_sb[:],
            )

        ctx.enter_context(tc.manual_schedule())
        half = TILES // 2
        keys = per_head.tile([P, TOKENS], BF16)
        queries = per_head.tile([P, TOKENS], BF16)
        kT[0], qT[0] = keys, queries
        flip_piece(k_rows, keys, 0, half, nc.vector.tensor_copy, psum_misc, "misc")
        flip_piece(q_rows, queries, 0, 1, nc.scalar.copy, psum_misc, "misc")
        flip_piece(k_rows, keys, half, TILES, nc.vector.tensor_copy, psum_e, "e_flip")
        scores(0)
        flip_piece(q_rows, queries, 1, TILES, nc.scalar.copy, psum_misc, "misc")
        negate_scores(0)
        group_values(0)
        for n in range(1, LEAD_S):
            scores(n)
        for n in range(1, LEAD_M):
            negate_scores(n)
        for n in range(tiles + 1):
            head, j = divmod(n, TILES)
            inside = n < tiles
            first = inside and head == 0
            prepare = inside and head + 1 < len(heads)
            r, phase = divmod(n, ROUND)
            if inside:
                exponentials(n)
            if n > 0:
                flip_exponentials(n - 1)
            if n + LEAD_S < tiles:
                scores(n + LEAD_S)
            if n < CHUNKS:
                for pair in range(PACK // 2):
                    flip_weights(n, pair)
            if prepare and j == 2:
                flip_rows(head + 1, k_rows, kT_flips)
            if prepare and j == 4:
                flip_rows(head + 1, q_rows, qT_flips)
            if first and j in (4, 5):
                mix_values(0, j - 4)
            if prepare and j == 6:
                mix_values(head + 1, 0)
            if inside and head > 0 and j == 2:
                mix_values(head, 1)
            if phase == 0 and r >= 2:
                weighted_sums(r - 2, 0, ROUND)
            if 0 < n <= tiles - LAST_ON_VECTOR:
                regroup_exponentials(n - 1, nc.scalar.copy)
            if prepare and j == 2:
                copy_keys(head + 1, 0, nc.scalar.copy)
            if prepare and j == 4:
                copy_queries(head + 1, nc.scalar.copy)
            if first and j == 4:
                copy_mixed(0, 0)
            if prepare and j == 6:
                copy_mixed(head + 1, 0)
            if j == 1 and head > 0:
                invert_sums(head - 1)
            if n + LEAD_M < tiles:
                negate_scores(n + LEAD_M)
            if n > tiles - LAST_ON_VECTOR:
                regroup_exponentials(n - 1, nc.vector.tensor_copy)
            if 1 <= n <= CHUNKS:
                for pair in range(PACK // 2):
                    group_weights(n - 1, pair)
            if first and j in (5, 6):
                add_bias(0, j - 5)
            if prepare and j == 7:
                add_bias(head + 1, 0)
            if prepare and j == 3:
                copy_keys(head + 1, 1, nc.vector.tensor_copy)
            if inside and head > 0 and j == 3:
                add_bias(head, 1)
            if phase == 1 and r >= 2:
                normalise(r - 2, 0, ROUND)
            if 2 <= n < 2 + CHUNKS:
                quantise_weights(n - 2)
            if n == 3:
                quantise_values(0)
            if phase == 2 and r >= 1:
                quantise_exponentials(r - 1, 0, ROUND)
            if inside and j == 7:
                quantise_mixed(head)
            if prepare and j == 4:
                quantise_values(head + 1)
            if prepare and j == 3:
                group_values(head + 1)
            if j == TILES - 1 and head + AHEAD < len(heads):
                load_head(head + AHEAD)
        last = rounds - 1
        quantise_exponentials(last, 0, PAIR)
        invert_sums(len(heads) - 1)
        normalise(last - 1, 0, ROUND)
        quantise_exponentials(last, PAIR, ROUND - 1)
        weighted_sums(last, 0, ROUND - 1)
        quantise_exponentials(last, ROUND - 1, ROUND)
        weighted_sums(last, ROUND - 1, ROUND)
        normalise(last, 0, ROUND - 1)
        normalise(last, ROUND - 1, ROUND)
